import numpy as np
import ml_dtypes


def mxq(x, axis, fmt="e4m3"):
    dtype, down = {"e4m3": (ml_dtypes.float8_e4m3fn, 7), "e5m2": (ml_dtypes.float8_e5m2, 14)}[fmt]
    v = np.moveaxis(np.asarray(x, np.float32).astype(ml_dtypes.bfloat16).astype(np.float64), axis, -1)
    blocks = v.reshape(v.shape[:-1] + (-1, 32))
    amax = np.abs(blocks).max(-1, keepdims=True)
    byte = np.maximum(np.where(amax > 0, np.frexp(amax)[1] - 1 + 127, 0) - down, 1)
    scale = np.exp2(byte - 127.0)
    codes = (blocks / scale).astype(np.float32).astype(dtype).astype(np.float64)
    return np.moveaxis((codes * scale).reshape(v.shape), -1, axis)


WIDE = False


def mx_kscale(k):
    if not WIDE:
        return np.ones(k)
    levels = np.array([10, -10, 5, -5, 0])
    a = np.random.permutation(np.resize(levels, k // 512 * 4)).reshape(k // 512, 4)
    idx = np.arange(k)
    return np.exp2(a[idx // 512, idx % 128 // 32])


BF16 = ml_dtypes.bfloat16


def bf(x):
    return np.asarray(x, np.float32).astype(BF16)


def f64(x):
    return np.asarray(x).astype(np.float64)


B, H, W, C, F, KH, KW, G, P = 4, 16, 18, 128, 512, 3, 3, 5, 3
HO, WO = H - KH + 1, W - KW + 1
NB = G + P
IN = KH * KW * C
GRID_MIN, GRID_MAX = -1.0, 1.0


def knots():
    h = (GRID_MAX - GRID_MIN) / G
    return np.linspace(GRID_MIN - P * h, GRID_MAX + P * h, G + 2 * P + 1)


def spline_basis(v):
    t = knots()
    v = v[..., None]
    b = np.where((v >= t[:-1]) & (v < t[1:]), 1.0, 0.0)
    for k in range(1, P + 1):
        b = ((v - t[:-(k + 1)]) / (t[k:-1] - t[:-(k + 1)]) * b[..., :-1]
             + (t[k + 1:] - v) / (t[k + 1:] - t[1:-k]) * b[..., 1:])
    return b


def setup_inputs():
    t = knots()
    a = np.maximum(np.log2(mx_kscale(C * NB)[::NB]), 0.0)
    x0 = np.random.standard_normal((B, H, W, C))
    sgn = np.where(np.random.standard_normal((B, H, W, C)) < 0.0, -1.0, 1.0)
    edge = sgn * (t[-1] - (t[1] - t[0]) * 2.0 ** (-a / 2.0))
    x = bf(np.where(a > 0.0, edge, x0))
    peak = spline_basis(f64(x)).max(axis=-1).reshape(B * H * W, C).max(axis=0)
    r = np.where(a > 0.0, 2.0 ** np.round(-np.log2(peak)), 1.0)
    rows = np.tile(r, KH * KW)
    return {"x": x,
            "spline_kernel": bf(np.random.standard_normal((IN, NB, F)) * rows[:, None, None]),
            "scale_factor": bf(np.random.standard_normal((IN, F)) / np.sqrt(IN)),
            "base": bf(np.random.standard_normal((B, HO, WO, F)) * 0.6),
            "kan_bias": bf(np.random.standard_normal(F) * 0.2),
            "conv_bias": bf(np.random.standard_normal(F) * 0.2)}


def reference(x, spline_kernel, scale_factor, base, kan_bias, conv_bias):
    sb = spline_basis(f64(x))
    sq = mxq(sb.reshape(B * H * W, C * NB), 1, "e4m3").reshape(B, H, W, C * NB)
    w = f64(spline_kernel) * f64(scale_factor)[:, None, :]
    wq = mxq(w.reshape(KH * KW, C * NB, F), 1, "e4m3")
    spl = 0.0
    for di in range(KH):
        for dj in range(KW):
            win = sq[:, di:di + HO, dj:dj + WO, :].reshape(B * HO * WO, C * NB)
            spl = spl + (win @ wq[di * KW + dj])
    out = spl.reshape(B, HO, WO, F) + f64(base) + f64(kan_bias)
    return out + f64(conv_bias)

@@ -1,0 +1,320 @@
+import math
+from contextlib import ExitStack
+
+import concourse.mybir as mybir
+from concourse.masks import make_identity
+
+FP8X4 = mybir.dt.float8_e4m3fn_x4
+BF16 = mybir.dt.bfloat16
+F32 = mybir.dt.float32
+I32 = mybir.dt.int32
+U32 = mybir.dt.uint32
+U8 = mybir.dt.uint8
+ALU = mybir.AluOpType
+ACT = mybir.ActivationFunctionType
+
+P = 128
+PACK = 4
+IMAGES, ROWS_IN, COLS_IN, CHANNELS = 4, 16, 18, 128
+ROWS_OUT, COLS_OUT, FEATURES = 14, 16, 512
+TAPS_H, TAPS_W = 3, 3
+HALVES = 2
+HALF_CHANNELS = CHANNELS // HALVES
+PIXELS = ROWS_IN * COLS_IN
+COLUMNS = PIXELS * IMAGES
+ROW_PITCH = COLS_IN * IMAGES
+ROW_WINDOW = COLS_OUT * IMAGES
+X_TILES = COLUMNS // P
+OUT_TILES = ROWS_OUT // 2
+SLICES = 6
+SLICE_COLUMNS = COLUMNS // SLICES
+SPREAD_N = SLICE_COLUMNS * PACK // 2
+SCALE_TAPS = 3
+RAW_BUFS = 3
+PASSES = TAPS_H * TAPS_W * HALVES
+BANDS = 2
+BAND_ROWS = ROWS_IN // BANDS
+BAND_COLUMNS = COLUMNS // BANDS
+VECTOR_EVERY = 4
+FLOPS = 2 * IMAGES * ROWS_OUT * COLS_OUT * TAPS_H * TAPS_W * CHANNELS * 8 * FEATURES
+
+
+def tile_conv2dkan_pa_kernel(tc, x, spline_kernel, scale_factor, base, kan_bias, conv_bias, out):
+    nc = tc.nc
+    with ExitStack() as ctx:
+        ctx.enter_context(tc.manual_schedule())
+        keep = ctx.enter_context(tc.tile_pool(name="keep", bufs=1))
+        work = ctx.enter_context(tc.tile_pool(name="work", bufs=3))
+        raw_pool = ctx.enter_context(tc.tile_pool(name="raw", bufs=RAW_BUFS))
+        weight_pool = ctx.enter_context(tc.tile_pool(name="weight", bufs=4))
+        scale_pool = ctx.enter_context(tc.tile_pool(name="scale", bufs=2))
+        code_pool = ctx.enter_context(tc.tile_pool(name="code", bufs=4))
+
+        x_sb = keep.tile([P, X_TILES, CHANNELS], BF16)
+        for b in range(IMAGES):
+            nc.sync.dma_start(
+                out=x_sb[b:P:IMAGES, :, :],
+                in_=x[b].rearrange("r q c -> (r q) c").rearrange("(i s) c -> s i c", s=P // IMAGES),
+            )
+        raw_of = {}
+        scale_of = {}
+
+        def load_weights(tap):
+            if tap % SCALE_TAPS == 0:
+                scale_rows = scale_pool.tile([P, SCALE_TAPS * HALVES, FEATURES], BF16, name="scale_rows")
+                for e in range(2):
+                    nc.sync.dma_start(
+                        out=scale_rows[e:P:2, :, :],
+                        in_=scale_factor[tap * CHANNELS : (tap + SCALE_TAPS) * CHANNELS].rearrange(
+                            "(n c) o -> c n o", c=HALF_CHANNELS
+                        ),
+                    )
+                scale_of[tap // SCALE_TAPS] = scale_rows
+            raw = raw_pool.tile([P, HALVES, PACK, FEATURES], BF16, name="raw")
+            nc.sync.dma_start(
+                out=raw[:],
+                in_=spline_kernel[tap * CHANNELS : (tap + 1) * CHANNELS]
+                .rearrange("c k o -> (c k) o")
+                .rearrange("(g p j) o -> p g j o", g=HALVES, j=PACK),
+            )
+            raw_of[tap] = raw
+
+        for tap in range(RAW_BUFS):
+            load_weights(tap)
+        bias_rows = keep.tile([P, FEATURES], BF16)
+        nc.vector.memset(bias_rows[:], 0.0)
+        nc.sync.dma_start(out=bias_rows[0:1, :], in_=kan_bias.rearrange("(a o) -> a o", a=1))
+        nc.sync.dma_start(out=bias_rows[1:2, :], in_=conv_bias.rearrange("(a o) -> a o", a=1))
+        base_sb = keep.tile([P, OUT_TILES, FEATURES], BF16)
+        for b in range(IMAGES):
+            nc.sync.dma_start(
+                out=base_sb[b:P:IMAGES, :, :],
+                in_=base[b].rearrange("p q o -> (p q) o").rearrange("(m s) o -> s m o", s=P // IMAGES),
+            )
+
+        ident = keep.tile([P, P], BF16)
+        make_identity(nc, ident[:])
+        ones = keep.tile([P, P], BF16)
+        nc.vector.memset(ones[:], 1.0)
+        spread = keep.tile([P, HALVES, HALF_CHANNELS, 2], BF16)
+        for g in range(HALVES):
+            own = ident[:, g * HALF_CHANNELS : (g + 1) * HALF_CHANNELS]
+            nc.vector.tensor_scalar(out=spread[:, g, :, 0], in0=own, scalar1=-1.0, scalar2=None, op0=ALU.mult)
+            nc.vector.tensor_copy(out=spread[:, g, :, 1], in_=own)
+
+        basis_bf = keep.tile([P, HALVES, COLUMNS * PACK], BF16, align_bytes=64)
+        basis_codes = keep.tile([P, HALVES, COLUMNS], U32, align_bytes=64)
+        basis_scales = keep.tile([P, HALVES, COLUMNS], U8, align_bytes=64)
+        nc.vector.memset(basis_scales[:].bitcast(I32), 0)
+        tap_codes = [
+            keep.tile([P, HALVES, ROWS_IN * ROW_WINDOW], U32, name="tap_codes%d" % dj, align_bytes=64)
+            for dj in range(TAPS_W)
+        ]
+        tap_scales = [
+            keep.tile([P, HALVES, ROWS_IN * ROW_WINDOW], U8, name="tap_scales%d" % dj, align_bytes=64)
+            for dj in range(TAPS_W)
+        ]
+        rest = keep.tile([P, OUT_TILES, FEATURES], F32)
+        x_t = keep.tile([P, COLUMNS], BF16)
+
+        scaled_of = {}
+        grouped_of = {}
+        codes_of = {}
+
+        def by_vector(n):
+            return n % VECTOR_EVERY == VECTOR_EVERY - 1
+
+        def scale_weights(n):
+            tap, g = divmod(n, HALVES)
+            factors = scale_of[tap // SCALE_TAPS][:, n % (SCALE_TAPS * HALVES), :]
+            if by_vector(n):
+                grouped = weight_pool.tile([P, FEATURES, PACK], BF16, name="grouped", align_bytes=64)
+                nc.vector.tensor_tensor(
+                    out=grouped[:],
+                    in0=raw_of[tap][:, g].rearrange("p j o -> p o j"),
+                    in1=factors.unsqueeze(2).to_broadcast([P, FEATURES, PACK]),
+                    op=ALU.mult,
+                )
+                grouped_of[n] = grouped
+            else:
+                scaled = weight_pool.tile([P, PACK, FEATURES], BF16, name="scaled")
+                nc.vector.tensor_tensor(
+                    out=scaled[:],
+                    in0=raw_of[tap][:, g],
+                    in1=factors.unsqueeze(1).to_broadcast([P, PACK, FEATURES]),
+                    op=ALU.mult,
+                )
+                scaled_of[n] = scaled
+
+        def regroup_weights(n):
+            if not by_vector(n):
+                grouped = weight_pool.tile([P, FEATURES, PACK], BF16, name="grouped", align_bytes=64)
+                nc.scalar.copy(
+                    out=grouped[:].rearrange("p (c i) j -> p c j i", i=4),
+                    in_=scaled_of[n][:].rearrange("p j (c i) -> p c j i", i=4),
+                )
+                grouped_of[n] = grouped
+
+        def quantise_weights(n):
+            w_codes = code_pool.tile([P, FEATURES], U32, name="w_codes", align_bytes=64)
+            w_scales = code_pool.tile([P, FEATURES], U8, name="w_scales", align_bytes=64)
+            nc.vector.quantize_mx(
+                out=w_codes[:].bitcast(FP8X4),
+                scales=w_scales[:],
+                in_=grouped_of[n][:].rearrange("p o j -> p (o j)"),
+            )
+            codes_of[n] = (w_codes, w_scales)
+
+        with tc.psum_pool(name="early", bufs=1) as early, tc.psum_pool(name="spreadp", bufs=6) as spread_psum:
+            for j in range(3):
+                x_t_ps = early.tile([P, 3, P], BF16)
+                for i in range(3):
+                    nc.tensor.transpose(out=x_t_ps[:, i, :], in_=x_sb[:, 3 * j + i, :], identity=ident[:])
+                nc.vector.tensor_copy(
+                    out=x_t[:, 3 * j * P : 3 * (j + 1) * P], in_=x_t_ps[:].rearrange("c i s -> c (i s)")
+                )
+
+            outer_of = {}
+            inner_of = {}
+            both_of = {}
+
+            def distances(sl):
+                cols = slice(sl * SLICE_COLUMNS, (sl + 1) * SLICE_COLUMNS)
+                dist = work.tile([P, PACK, SLICE_COLUMNS], F32, name="dist")
+                for t in range(PACK):
+                    nc.scalar.activation(out=dist[:, t, :], in_=x_t[:, cols], func=ACT.Abs, bias=1.5 - t, scale=2.5)
+                nc.scalar.activation(out=dist[:], in_=dist[:], func=ACT.Abs, bias=-2.0, scale=1.0)
+                outer = work.tile([P, PACK, SLICE_COLUMNS], F32, name="outer")
+                nc.vector.tensor_scalar(out=outer[:], in0=dist[:], scalar1=2.0, scalar2=2.0, op0=ALU.min, op1=ALU.subtract)
+                nc.vector.tensor_scalar(out=dist[:], in0=dist[:], scalar1=1.0, scalar2=1.0, op0=ALU.min, op1=ALU.subtract)
+                outer_of[sl] = outer
+                inner_of[sl] = dist
+
+            def values(sl):
+                cols = slice(sl * SLICE_COLUMNS, (sl + 1) * SLICE_COLUMNS)
+                outer = outer_of[sl]
+                inner = inner_of[sl]
+                outer_cube = work.tile([P, PACK, SLICE_COLUMNS], F32, name="outer_cube")
+                nc.scalar.activation(out=outer_cube[:], in_=outer[:], func=ACT.Square, scale=math.sqrt(1.0 / 3.0))
+                inner_cube = work.tile([P, PACK, SLICE_COLUMNS], F32, name="inner_cube")
+                nc.scalar.activation(out=inner_cube[:], in_=inner[:], func=ACT.Square, scale=math.sqrt(4.0 / 3.0))
+                upper = work.tile([P, PACK, SLICE_COLUMNS], BF16, name="upper")
+                for t in range(PACK):
+                    nc.vector.tensor_scalar(
+                        out=upper[:, t, :], in0=x_t[:, cols], scalar1=2.5, scalar2=t - 1.5, op0=ALU.mult, op1=ALU.is_ge
+                    )
+                nc.vector.tensor_tensor(out=outer_cube[:], in0=outer_cube[:], in1=outer[:], op=ALU.mult)
+                nc.vector.tensor_tensor(out=inner_cube[:], in0=inner_cube[:], in1=inner[:], op=ALU.mult)
+                twice = work.tile([P, PACK, SLICE_COLUMNS], BF16, name="twice")
+                nc.vector.tensor_tensor(out=twice[:], in0=inner_cube[:], in1=outer_cube[:], op=ALU.subtract)
+                signed = work.tile([P, SLICE_COLUMNS, PACK], BF16, name="signed")
+                nc.vector.scalar_tensor_tensor(
+                    out=signed[:],
+                    in0=upper[:].rearrange("c t s -> c s t"),
+                    scalar=0.5,
+                    in1=twice[:].rearrange("c t s -> c s t"),
+                    op0=ALU.subtract,
+                    op1=ALU.mult,
+                )
+                signed_flat = signed[:].rearrange("c s t -> c (s t)")
+                for g in range(HALVES):
+                    for j in range(2):
+                        both = spread_psum.tile([P, SPREAD_N], F32, name="both")
+                        nc.tensor.matmul(
+                            out=both[:],
+                            lhsT=spread[:, g].rearrange("c a e -> c (a e)"),
+                            rhs=signed_flat[:, j * SPREAD_N : (j + 1) * SPREAD_N],
+                            start=True,
+                            stop=True,
+                        )
+                        both_of[(sl, g, j)] = both
+
+            def collect(sl):
+                for g in range(HALVES):
+                    for j in range(2):
+                        first = sl * SLICE_COLUMNS * PACK + j * SPREAD_N
+                        nc.scalar.activation(
+                            out=basis_bf[:, g, first : first + SPREAD_N], in_=both_of[(sl, g, j)][:], func=ACT.Relu
+                        )
+
+            def quantise_band(band):
+                for g in range(HALVES):
+                    for first, width in ((0, 512), (512, 64)):
+                        first = first + band * BAND_COLUMNS
+                        nc.vector.quantize_mx(
+                            out=basis_codes[:, g, first : first + width].bitcast(FP8X4),
+                            scales=basis_scales[:, g, first : first + width],
+                            in_=basis_bf[:, g, first * PACK : (first + width) * PACK],
+                        )
+                rows = slice(band * BAND_ROWS, (band + 1) * BAND_ROWS)
+                for dj in range(TAPS_W):
+                    nc.vector.tensor_copy(
+                        out=tap_codes[dj][:].bitcast(I32).rearrange("p g (r w) -> p g r w", w=ROW_WINDOW)[:, :, rows, :],
+                        in_=basis_codes[:].bitcast(I32).rearrange("p g (r w) -> p g r w", w=ROW_PITCH)[
+                            :, :, rows, dj * IMAGES : dj * IMAGES + ROW_WINDOW
+                        ],
+                    )
+                    nc.vector.tensor_copy(
+                        out=tap_scales[dj][:].bitcast(I32).rearrange("p g (r w) -> p g r w", w=ROW_WINDOW // 4)[:, :, rows, :],
+                        in_=basis_scales[:].bitcast(I32).rearrange("p g (r w) -> p g r w", w=ROW_PITCH // 4)[
+                            :, :, rows, dj : dj + ROW_WINDOW // 4
+                        ],
+                    )
+
+            for step in range(SLICES + 2):
+                if step < SLICES:
+                    distances(step)
+                if 1 <= step <= SLICES:
+                    values(step - 1)
+                if step >= 2:
+                    collect(step - 2)
+                if step - 2 == SLICES // BANDS - 1:
+                    quantise_band(0)
+            scale_weights(0)
+            scale_weights(1)
+            regroup_weights(0)
+            quantise_band(1)
+
+            bias_ps = early.tile([P, FEATURES], F32)
+            nc.tensor.matmul(out=bias_ps[:], lhsT=ones[:], rhs=bias_rows[:], start=True, stop=True)
+            bias_sb = keep.tile([P, FEATURES], F32)
+            nc.scalar.copy(out=bias_sb[:], in_=bias_ps[:])
+            nc.gpsimd.tensor_tensor(
+                out=rest[:],
+                in0=base_sb[:],
+                in1=bias_sb[:].unsqueeze(1).to_broadcast([P, OUT_TILES, FEATURES]),
+                op=ALU.add,
+            )
+
+        acc_pool = ctx.enter_context(tc.psum_pool(name="acc", bufs=1, reuse_waits="tile"))
+        acc = [acc_pool.tile([P, FEATURES], F32, name="acc%d" % m) for m in range(OUT_TILES)]
+        for n in range(PASSES):
+            tap, g = divmod(n, HALVES)
+            di, dj = divmod(tap, TAPS_W)
+            if n + 2 < PASSES:
+                scale_weights(n + 2)
+            if n + 1 < PASSES:
+                regroup_weights(n + 1)
+            quantise_weights(n)
+            w_codes, w_scales = codes_of[n]
+            for m in range(OUT_TILES):
+                window = slice((2 * m + di) * ROW_WINDOW, (2 * m + di) * ROW_WINDOW + P)
+                nc.tensor.matmul_mx(
+                    out=acc[m][:],
+                    lhsT=tap_codes[dj][:, g, window].bitcast(FP8X4),
+                    lhsT_scale=tap_scales[dj][:, g, window],
+                    rhs=w_codes[:].bitcast(FP8X4),
+                    rhs_scale=w_scales[:],
+                    start=(n == 0),
+                    stop=(n == PASSES - 1),
+                )
+            if g == HALVES - 1 and tap + RAW_BUFS < TAPS_H * TAPS_W:
+                load_weights(tap + RAW_BUFS)
+
+        for m in range(OUT_TILES):
+            nc.vector.tensor_tensor(out=rest[:, m, :], in0=acc[m][:], in1=rest[:, m, :], op=ALU.add)
+            for b in range(IMAGES):
+                nc.sync.dma_start(
+                    out=out[b].rearrange("p q o -> (p q) o")[m * 32 : (m + 1) * 32, :],
+                    in_=rest[b:P:IMAGES, m, :],
+                )

@@ -18,25 +18,24 @@ PACK = 4
 IMAGES, ROWS_IN, COLS_IN, CHANNELS = 4, 16, 18, 128
 ROWS_OUT, COLS_OUT, FEATURES = 14, 16, 512
 TAPS_H, TAPS_W = 3, 3
+TAPS = TAPS_H * TAPS_W
 HALVES = 2
-HALF_CHANNELS = CHANNELS // HALVES
-PIXELS = ROWS_IN * COLS_IN
-COLUMNS = PIXELS * IMAGES
+COLUMNS = ROWS_IN * COLS_IN * IMAGES
 ROW_PITCH = COLS_IN * IMAGES
 ROW_WINDOW = COLS_OUT * IMAGES
 X_TILES = COLUMNS // P
+TILE_VALUES = P * PACK
 OUT_TILES = ROWS_OUT // 2
-SLICES = 6
-SLICE_COLUMNS = COLUMNS // SLICES
-SPREAD_N = SLICE_COLUMNS * PACK // 2
-SCALE_TAPS = 3
-RAW_BUFS = 3
-PASSES = TAPS_H * TAPS_W * HALVES
-BANDS = 2
-BAND_ROWS = ROWS_IN // BANDS
-BAND_COLUMNS = COLUMNS // BANDS
-VECTOR_EVERY = 4
-FLOPS = 2 * IMAGES * ROWS_OUT * COLS_OUT * TAPS_H * TAPS_W * CHANNELS * 8 * FEATURES
+EARLY_TILES = 7
+EARLY_ROWS = EARLY_TILES * P // ROW_PITCH
+RUN = 16
+CHUNKS = TAPS * HALVES
+RAW_BUFS = 4
+AHEAD = 4
+VECTOR_EVERY = 9
+FIRST_SCALE_STEP = 2
+STAGES = 4
+FLOPS = 2 * IMAGES * ROWS_OUT * COLS_OUT * TAPS * CHANNELS * 8 * FEATURES
 
 
 def tile_conv2dkan_pa_kernel(tc, x, spline_kernel, scale_factor, base, kan_bias, conv_bias, out):
@@ -46,9 +45,14 @@ def tile_conv2dkan_pa_kernel(tc, x, spline_kernel, scale_factor, base, kan_bias,
         keep = ctx.enter_context(tc.tile_pool(name="keep", bufs=1))
         work = ctx.enter_context(tc.tile_pool(name="work", bufs=3))
         raw_pool = ctx.enter_context(tc.tile_pool(name="raw", bufs=RAW_BUFS))
-        weight_pool = ctx.enter_context(tc.tile_pool(name="weight", bufs=4))
-        scale_pool = ctx.enter_context(tc.tile_pool(name="scale", bufs=2))
+        weight_pool = ctx.enter_context(tc.tile_pool(name="weight", bufs=AHEAD + 2))
         code_pool = ctx.enter_context(tc.tile_pool(name="code", bufs=4))
+
+        def partitions_of_run(first):
+            a, b = divmod(first // RUN, 2)
+            return slice(2 * RUN * a + b, 2 * RUN * (a + 1), 2)
+
+        channel_runs = [(partitions_of_run(first), first) for first in range(0, CHANNELS, RUN)]
 
         x_sb = keep.tile([P, X_TILES, CHANNELS], BF16)
         for b in range(IMAGES):
@@ -56,31 +60,26 @@ def tile_conv2dkan_pa_kernel(tc, x, spline_kernel, scale_factor, base, kan_bias,
                 out=x_sb[b:P:IMAGES, :, :],
                 in_=x[b].rearrange("r q c -> (r q) c").rearrange("(i s) c -> s i c", s=P // IMAGES),
             )
+        factors = keep.tile([P, TAPS, FEATURES], BF16)
+        for partitions, first in channel_runs:
+            nc.sync.dma_start(
+                out=factors[partitions, :, :],
+                in_=scale_factor.rearrange("(tap c) o -> c tap o", c=CHANNELS)[first : first + RUN],
+            )
+
         raw_of = {}
-        scale_of = {}
 
         def load_weights(tap):
-            if tap % SCALE_TAPS == 0:
-                scale_rows = scale_pool.tile([P, SCALE_TAPS * HALVES, FEATURES], BF16, name="scale_rows")
-                for e in range(2):
-                    nc.sync.dma_start(
-                        out=scale_rows[e:P:2, :, :],
-                        in_=scale_factor[tap * CHANNELS : (tap + SCALE_TAPS) * CHANNELS].rearrange(
-                            "(n c) o -> c n o", c=HALF_CHANNELS
-                        ),
-                    )
-                scale_of[tap // SCALE_TAPS] = scale_rows
-            raw = raw_pool.tile([P, HALVES, PACK, FEATURES], BF16, name="raw")
-            nc.sync.dma_start(
-                out=raw[:],
-                in_=spline_kernel[tap * CHANNELS : (tap + 1) * CHANNELS]
-                .rearrange("c k o -> (c k) o")
-                .rearrange("(g p j) o -> p g j o", g=HALVES, j=PACK),
-            )
+            raw = raw_pool.tile([P, HALVES * PACK, FEATURES], BF16, name="raw")
+            for partitions, first in channel_runs:
+                nc.sync.dma_start(
+                    out=raw[partitions, :, :],
+                    in_=spline_kernel[tap * CHANNELS + first : tap * CHANNELS + first + RUN],
+                )
             raw_of[tap] = raw
 
-        for tap in range(RAW_BUFS):
-            load_weights(tap)
+        load_weights(0)
+        load_weights(1)
         bias_rows = keep.tile([P, FEATURES], BF16)
         nc.vector.memset(bias_rows[:], 0.0)
         nc.sync.dma_start(out=bias_rows[0:1, :], in_=kan_bias.rearrange("(a o) -> a o", a=1))
@@ -91,16 +90,20 @@ def tile_conv2dkan_pa_kernel(tc, x, spline_kernel, scale_factor, base, kan_bias,
                 out=base_sb[b:P:IMAGES, :, :],
                 in_=base[b].rearrange("p q o -> (p q) o").rearrange("(m s) o -> s m o", s=P // IMAGES),
             )
+        for tap in range(2, RAW_BUFS):
+            load_weights(tap)
 
         ident = keep.tile([P, P], BF16)
         make_identity(nc, ident[:])
         ones = keep.tile([P, P], BF16)
         nc.vector.memset(ones[:], 1.0)
-        spread = keep.tile([P, HALVES, HALF_CHANNELS, 2], BF16)
-        for g in range(HALVES):
-            own = ident[:, g * HALF_CHANNELS : (g + 1) * HALF_CHANNELS]
-            nc.vector.tensor_scalar(out=spread[:, g, :, 0], in0=own, scalar1=-1.0, scalar2=None, op0=ALU.mult)
-            nc.vector.tensor_copy(out=spread[:, g, :, 1], in_=own)
+        stretch = keep.tile([P, P, PACK], BF16)
+        nc.vector.tensor_scalar(
+            out=stretch[:], in0=ident[:].unsqueeze(2).to_broadcast([P, P, PACK]), scalar1=2.5, scalar2=None, op0=ALU.mult
+        )
+        shift = keep.tile([P, P, PACK], BF16)
+        for t in range(PACK):
+            nc.vector.memset(shift[:, :, t], (1.5 - t) / P)
 
         basis_bf = keep.tile([P, HALVES, COLUMNS * PACK], BF16, align_bytes=64)
         basis_codes = keep.tile([P, HALVES, COLUMNS], U32, align_bytes=64)
@@ -115,7 +118,16 @@ def tile_conv2dkan_pa_kernel(tc, x, spline_kernel, scale_factor, base, kan_bias,
             for dj in range(TAPS_W)
         ]
         rest = keep.tile([P, OUT_TILES, FEATURES], F32)
-        x_t = keep.tile([P, COLUMNS], BF16)
+
+        x_sorted = keep.tile([P, X_TILES, CHANNELS], BF16)
+        nc.vector.tensor_scalar(
+            out=x_sorted[:].rearrange("s i (a c b) -> s (i a) c b", c=RUN, b=2),
+            in0=x_sb[:].rearrange("s i (a b c) -> s (i a) c b", b=2, c=RUN),
+            scalar1=-4.0,
+            scalar2=4.0,
+            op0=ALU.max,
+            op1=ALU.min,
+        )
 
         scaled_of = {}
         grouped_of = {}
@@ -125,14 +137,14 @@ def tile_conv2dkan_pa_kernel(tc, x, spline_kernel, scale_factor, base, kan_bias,
             return n % VECTOR_EVERY == VECTOR_EVERY - 1
 
         def scale_weights(n):
-            tap, g = divmod(n, HALVES)
-            factors = scale_of[tap // SCALE_TAPS][:, n % (SCALE_TAPS * HALVES), :]
+            tap, half = divmod(n, HALVES)
+            rows = raw_of[tap][:, half * PACK : (half + 1) * PACK, :]
             if by_vector(n):
                 grouped = weight_pool.tile([P, FEATURES, PACK], BF16, name="grouped", align_bytes=64)
                 nc.vector.tensor_tensor(
                     out=grouped[:],
-                    in0=raw_of[tap][:, g].rearrange("p j o -> p o j"),
-                    in1=factors.unsqueeze(2).to_broadcast([P, FEATURES, PACK]),
+                    in0=rows.rearrange("p j o -> p o j"),
+                    in1=factors[:, tap, :].unsqueeze(2).to_broadcast([P, FEATURES, PACK]),
                     op=ALU.mult,
                 )
                 grouped_of[n] = grouped
@@ -140,11 +152,13 @@ def tile_conv2dkan_pa_kernel(tc, x, spline_kernel, scale_factor, base, kan_bias,
                 scaled = weight_pool.tile([P, PACK, FEATURES], BF16, name="scaled")
                 nc.vector.tensor_tensor(
                     out=scaled[:],
-                    in0=raw_of[tap][:, g],
-                    in1=factors.unsqueeze(1).to_broadcast([P, PACK, FEATURES]),
+                    in0=rows,
+                    in1=factors[:, tap, :].unsqueeze(1).to_broadcast([P, PACK, FEATURES]),
                     op=ALU.mult,
                 )
                 scaled_of[n] = scaled
+            if half == HALVES - 1 and tap + RAW_BUFS < TAPS:
+                load_weights(tap + RAW_BUFS)
 
         def regroup_weights(n):
             if not by_vector(n):
@@ -165,153 +179,214 @@ def tile_conv2dkan_pa_kernel(tc, x, spline_kernel, scale_factor, base, kan_bias,
             )
             codes_of[n] = (w_codes, w_scales)
 
-        with tc.psum_pool(name="early", bufs=1) as early, tc.psum_pool(name="spreadp", bufs=6) as spread_psum:
-            for j in range(3):
-                x_t_ps = early.tile([P, 3, P], BF16)
-                for i in range(3):
-                    nc.tensor.transpose(out=x_t_ps[:, i, :], in_=x_sb[:, 3 * j + i, :], identity=ident[:])
-                nc.vector.tensor_copy(
-                    out=x_t[:, 3 * j * P : 3 * (j + 1) * P], in_=x_t_ps[:].rearrange("c i s -> c (i s)")
-                )
+        def quantise_basis(first_column, widths):
+            for half in range(HALVES):
+                first = first_column
+                for width in widths:
+                    nc.vector.quantize_mx(
+                        out=basis_codes[:, half, first : first + width].bitcast(FP8X4),
+                        scales=basis_scales[:, half, first : first + width],
+                        in_=basis_bf[:, half, first * PACK : (first + width) * PACK],
+                    )
+                    first = first + width
 
+        def copy_tap(dj, first_row, end_row):
+            rows = slice(first_row, end_row)
+            nc.vector.tensor_copy(
+                out=tap_codes[dj][:].bitcast(I32).rearrange("p h (r w) -> p h r w", w=ROW_WINDOW)[:, :, rows, :],
+                in_=basis_codes[:].bitcast(I32).rearrange("p h (r w) -> p h r w", w=ROW_PITCH)[
+                    :, :, rows, dj * IMAGES : dj * IMAGES + ROW_WINDOW
+                ],
+            )
+            nc.vector.tensor_copy(
+                out=tap_scales[dj][:].bitcast(I32).rearrange("p h (r w) -> p h r w", w=ROW_WINDOW // 4)[:, :, rows, :],
+                in_=basis_scales[:].bitcast(I32).rearrange("p h (r w) -> p h r w", w=ROW_PITCH // 4)[
+                    :, :, rows, dj : dj + ROW_WINDOW // 4
+                ],
+            )
+
+        bias_psum = ctx.enter_context(tc.psum_pool(name="bias", bufs=1))
+        with tc.psum_pool(name="offsets", bufs=4) as offset_psum:
+            offset_of = {}
+            dist_of = {}
+            side_of = {}
             outer_of = {}
             inner_of = {}
-            both_of = {}
+            outer_cube_of = {}
+            inner_cube_of = {}
+            value_of = {}
+            signed_of = {}
 
-            def distances(sl):
-                cols = slice(sl * SLICE_COLUMNS, (sl + 1) * SLICE_COLUMNS)
-                dist = work.tile([P, PACK, SLICE_COLUMNS], F32, name="dist")
-                for t in range(PACK):
-                    nc.scalar.activation(out=dist[:, t, :], in_=x_t[:, cols], func=ACT.Abs, bias=1.5 - t, scale=2.5)
-                nc.scalar.activation(out=dist[:], in_=dist[:], func=ACT.Abs, bias=-2.0, scale=1.0)
-                outer = work.tile([P, PACK, SLICE_COLUMNS], F32, name="outer")
-                nc.vector.tensor_scalar(out=outer[:], in0=dist[:], scalar1=2.0, scalar2=2.0, op0=ALU.min, op1=ALU.subtract)
-                nc.vector.tensor_scalar(out=dist[:], in0=dist[:], scalar1=1.0, scalar2=1.0, op0=ALU.min, op1=ALU.subtract)
-                outer_of[sl] = outer
-                inner_of[sl] = dist
-
-            def values(sl):
-                cols = slice(sl * SLICE_COLUMNS, (sl + 1) * SLICE_COLUMNS)
-                outer = outer_of[sl]
-                inner = inner_of[sl]
-                outer_cube = work.tile([P, PACK, SLICE_COLUMNS], F32, name="outer_cube")
-                nc.scalar.activation(out=outer_cube[:], in_=outer[:], func=ACT.Square, scale=math.sqrt(1.0 / 3.0))
-                inner_cube = work.tile([P, PACK, SLICE_COLUMNS], F32, name="inner_cube")
-                nc.scalar.activation(out=inner_cube[:], in_=inner[:], func=ACT.Square, scale=math.sqrt(4.0 / 3.0))
-                upper = work.tile([P, PACK, SLICE_COLUMNS], BF16, name="upper")
-                for t in range(PACK):
-                    nc.vector.tensor_scalar(
-                        out=upper[:, t, :], in0=x_t[:, cols], scalar1=2.5, scalar2=t - 1.5, op0=ALU.mult, op1=ALU.is_ge
-                    )
-                nc.vector.tensor_tensor(out=outer_cube[:], in0=outer_cube[:], in1=outer[:], op=ALU.mult)
-                nc.vector.tensor_tensor(out=inner_cube[:], in0=inner_cube[:], in1=inner[:], op=ALU.mult)
-                twice = work.tile([P, PACK, SLICE_COLUMNS], BF16, name="twice")
-                nc.vector.tensor_tensor(out=twice[:], in0=inner_cube[:], in1=outer_cube[:], op=ALU.subtract)
-                signed = work.tile([P, SLICE_COLUMNS, PACK], BF16, name="signed")
-                nc.vector.scalar_tensor_tensor(
-                    out=signed[:],
-                    in0=upper[:].rearrange("c t s -> c s t"),
-                    scalar=0.5,
-                    in1=twice[:].rearrange("c t s -> c s t"),
-                    op0=ALU.subtract,
-                    op1=ALU.mult,
+            def offsets(i):
+                offset = offset_psum.tile([P, TILE_VALUES], F32, name="offset")
+                nc.tensor.matmul(
+                    out=offset[:], lhsT=x_sorted[:, i, :], rhs=stretch[:].rearrange("s c t -> s (c t)"), start=True, stop=False
                 )
-                signed_flat = signed[:].rearrange("c s t -> c (s t)")
-                for g in range(HALVES):
-                    for j in range(2):
-                        both = spread_psum.tile([P, SPREAD_N], F32, name="both")
-                        nc.tensor.matmul(
-                            out=both[:],
-                            lhsT=spread[:, g].rearrange("c a e -> c (a e)"),
-                            rhs=signed_flat[:, j * SPREAD_N : (j + 1) * SPREAD_N],
-                            start=True,
-                            stop=True,
-                        )
-                        both_of[(sl, g, j)] = both
+                nc.tensor.matmul(
+                    out=offset[:], lhsT=ones[:], rhs=shift[:].rearrange("s c t -> s (c t)"), start=False, stop=True
+                )
+                offset_of[i] = offset
 
-            def collect(sl):
-                for g in range(HALVES):
-                    for j in range(2):
-                        first = sl * SLICE_COLUMNS * PACK + j * SPREAD_N
-                        nc.scalar.activation(
-                            out=basis_bf[:, g, first : first + SPREAD_N], in_=both_of[(sl, g, j)][:], func=ACT.Relu
-                        )
+            def fold(i):
+                dist_of[i] = work.tile([P, TILE_VALUES], F32, name="dist")
+                nc.scalar.activation(out=dist_of[i][:], in_=offset_of[i][:], func=ACT.Abs)
 
-            def quantise_band(band):
-                for g in range(HALVES):
-                    for first, width in ((0, 512), (512, 64)):
-                        first = first + band * BAND_COLUMNS
-                        nc.vector.quantize_mx(
-                            out=basis_codes[:, g, first : first + width].bitcast(FP8X4),
-                            scales=basis_scales[:, g, first : first + width],
-                            in_=basis_bf[:, g, first * PACK : (first + width) * PACK],
-                        )
-                rows = slice(band * BAND_ROWS, (band + 1) * BAND_ROWS)
-                for dj in range(TAPS_W):
-                    nc.vector.tensor_copy(
-                        out=tap_codes[dj][:].bitcast(I32).rearrange("p g (r w) -> p g r w", w=ROW_WINDOW)[:, :, rows, :],
-                        in_=basis_codes[:].bitcast(I32).rearrange("p g (r w) -> p g r w", w=ROW_PITCH)[
-                            :, :, rows, dj * IMAGES : dj * IMAGES + ROW_WINDOW
-                        ],
-                    )
-                    nc.vector.tensor_copy(
-                        out=tap_scales[dj][:].bitcast(I32).rearrange("p g (r w) -> p g r w", w=ROW_WINDOW // 4)[:, :, rows, :],
-                        in_=basis_scales[:].bitcast(I32).rearrange("p g (r w) -> p g r w", w=ROW_PITCH // 4)[
-                            :, :, rows, dj : dj + ROW_WINDOW // 4
-                        ],
-                    )
+            def side(i):
+                side_of[i] = work.tile([P, TILE_VALUES], BF16, name="side")
+                nc.scalar.activation(out=side_of[i][:], in_=offset_of[i][:], func=ACT.Sign)
 
-            for step in range(SLICES + 2):
-                if step < SLICES:
-                    distances(step)
-                if 1 <= step <= SLICES:
-                    values(step - 1)
-                if step >= 2:
-                    collect(step - 2)
-                if step - 2 == SLICES // BANDS - 1:
-                    quantise_band(0)
-            scale_weights(0)
-            scale_weights(1)
+            def distance(i):
+                nc.scalar.activation(out=dist_of[i][:], in_=dist_of[i][:], func=ACT.Abs, bias=-2.0, scale=1.0)
+
+            def outer(i):
+                outer_of[i] = work.tile([P, TILE_VALUES], F32, name="outer")
+                nc.scalar.activation(out=outer_of[i][:], in_=dist_of[i][:], func=ACT.Relu, bias=2.0, scale=-1.0)
+
+            def outer_square(i):
+                outer_cube_of[i] = work.tile([P, TILE_VALUES], F32, name="outer_cube")
+                nc.scalar.activation(
+                    out=outer_cube_of[i][:], in_=outer_of[i][:], func=ACT.Square, scale=math.sqrt(1.0 / 6.0)
+                )
+
+            def inner_square(i):
+                inner_cube_of[i] = work.tile([P, TILE_VALUES], F32, name="inner_cube")
+                nc.scalar.activation(
+                    out=inner_cube_of[i][:],
+                    in_=dist_of[i][:],
+                    func=ACT.Square,
+                    bias=math.sqrt(2.0 / 3.0),
+                    scale=-math.sqrt(2.0 / 3.0),
+                )
+
+            def inner(i):
+                inner_of[i] = work.tile([P, TILE_VALUES], F32, name="inner")
+                nc.vector.tensor_scalar(
+                    out=inner_of[i][:], in0=dist_of[i][:], scalar1=1.0, scalar2=1.0, op0=ALU.min, op1=ALU.subtract
+                )
+
+            def outer_cube(i):
+                nc.vector.tensor_tensor(out=outer_cube_of[i][:], in0=outer_cube_of[i][:], in1=outer_of[i][:], op=ALU.mult)
+
+            def inner_cube(i):
+                nc.vector.tensor_tensor(out=inner_cube_of[i][:], in0=inner_cube_of[i][:], in1=inner_of[i][:], op=ALU.mult)
+
+            def value(i):
+                value_of[i] = work.tile([P, TILE_VALUES], BF16, name="value")
+                nc.vector.tensor_tensor(out=value_of[i][:], in0=outer_cube_of[i][:], in1=inner_cube_of[i][:], op=ALU.add)
+
+            def signed(i):
+                signed_of[i] = work.tile([P, TILE_VALUES], BF16, name="signed")
+                nc.vector.tensor_tensor(out=signed_of[i][:], in0=value_of[i][:], in1=side_of[i][:], op=ALU.mult)
+
+            def upper_half(i):
+                nc.vector.tensor_scalar(
+                    out=basis_bf[:, 1, i * TILE_VALUES : (i + 1) * TILE_VALUES],
+                    in0=signed_of[i][:],
+                    scalar1=0.0,
+                    scalar2=None,
+                    op0=ALU.max,
+                )
+
+            def lower_half(i):
+                nc.vector.tensor_scalar(
+                    out=basis_bf[:, 0, i * TILE_VALUES : (i + 1) * TILE_VALUES],
+                    in0=signed_of[i][:],
+                    scalar1=-1.0,
+                    scalar2=0.0,
+                    op0=ALU.mult,
+                    op1=ALU.max,
+                )
+
+            offsets(0)
+            offsets(1)
+            def live(i):
+                return 0 <= i < X_TILES
+
+            for step in range(X_TILES + STAGES - 1):
+                first, second, third, fourth = step, step - 1, step - 2, step - 3
+                if live(first + 2):
+                    offsets(first + 2)
+                if live(first):
+                    fold(first)
+                if live(second):
+                    outer(second)
+                if live(first):
+                    side(first)
+                if live(second):
+                    outer_square(second)
+                if live(first):
+                    distance(first)
+                if live(second):
+                    inner_square(second)
+                if live(third):
+                    outer_cube(third)
+                if live(second):
+                    inner(second)
+                if live(third):
+                    inner_cube(third)
+                if live(fourth):
+                    upper_half(fourth)
+                if live(third):
+                    value(third)
+                if live(fourth):
+                    lower_half(fourth)
+                if live(third):
+                    signed(third)
+                if fourth == EARLY_TILES - 1:
+                    quantise_basis(0, (512, 256, 128))
+                    copy_tap(0, 0, EARLY_ROWS)
+                if FIRST_SCALE_STEP <= step < FIRST_SCALE_STEP + AHEAD:
+                    scale_weights(step - FIRST_SCALE_STEP)
             regroup_weights(0)
-            quantise_band(1)
+            quantise_basis(EARLY_TILES * P, (256,))
+            copy_tap(0, EARLY_ROWS, ROWS_IN)
 
-            bias_ps = early.tile([P, FEATURES], F32)
-            nc.tensor.matmul(out=bias_ps[:], lhsT=ones[:], rhs=bias_rows[:], start=True, stop=True)
-            bias_sb = keep.tile([P, FEATURES], F32)
-            nc.scalar.copy(out=bias_sb[:], in_=bias_ps[:])
-            nc.gpsimd.tensor_tensor(
-                out=rest[:],
-                in0=base_sb[:],
-                in1=bias_sb[:].unsqueeze(1).to_broadcast([P, OUT_TILES, FEATURES]),
+        bias_ps = bias_psum.tile([P, FEATURES], F32)
+        nc.tensor.matmul(out=bias_ps[:], lhsT=ones[:], rhs=bias_rows[:], start=True, stop=True)
+
+        def add_biases(first_tile, end_tile):
+            nc.vector.tensor_tensor(
+                out=rest[:, first_tile:end_tile, :],
+                in0=base_sb[:, first_tile:end_tile, :],
+                in1=bias_ps[:].unsqueeze(1).to_broadcast([P, end_tile - first_tile, FEATURES]),
                 op=ALU.add,
             )
 
         acc_pool = ctx.enter_context(tc.psum_pool(name="acc", bufs=1, reuse_waits="tile"))
         acc = [acc_pool.tile([P, FEATURES], F32, name="acc%d" % m) for m in range(OUT_TILES)]
-        for n in range(PASSES):
-            tap, g = divmod(n, HALVES)
+
+        def multiply(n, m):
+            tap, half = divmod(n, HALVES)
             di, dj = divmod(tap, TAPS_W)
-            if n + 2 < PASSES:
-                scale_weights(n + 2)
-            if n + 1 < PASSES:
-                regroup_weights(n + 1)
-            quantise_weights(n)
+            window = slice((2 * m + di) * ROW_WINDOW, (2 * m + di) * ROW_WINDOW + P)
             w_codes, w_scales = codes_of[n]
-            for m in range(OUT_TILES):
-                window = slice((2 * m + di) * ROW_WINDOW, (2 * m + di) * ROW_WINDOW + P)
-                nc.tensor.matmul_mx(
-                    out=acc[m][:],
-                    lhsT=tap_codes[dj][:, g, window].bitcast(FP8X4),
-                    lhsT_scale=tap_scales[dj][:, g, window],
-                    rhs=w_codes[:].bitcast(FP8X4),
-                    rhs_scale=w_scales[:],
-                    start=(n == 0),
-                    stop=(n == PASSES - 1),
-                )
-            if g == HALVES - 1 and tap + RAW_BUFS < TAPS_H * TAPS_W:
-                load_weights(tap + RAW_BUFS)
+            nc.tensor.matmul_mx(
+                out=acc[m][:],
+                lhsT=tap_codes[dj][:, half, window].bitcast(FP8X4),
+                lhsT_scale=tap_scales[dj][:, half, window],
+                rhs=w_codes[:].bitcast(FP8X4),
+                rhs_scale=w_scales[:],
+                start=(n == 0),
+                stop=(n == CHUNKS - 1),
+            )
+
+        for n in range(CHUNKS):
+            quantise_weights(n)
+            if n + 1 < TAPS_W:
+                copy_tap(n + 1, 0, ROWS_IN)
+            if n + AHEAD < CHUNKS:
+                scale_weights(n + AHEAD)
+            if n + 1 < CHUNKS:
+                regroup_weights(n + 1)
+            if CHUNKS - AHEAD <= n < CHUNKS - AHEAD + 2:
+                add_biases(4 * (n - CHUNKS + AHEAD), min(4 * (n - CHUNKS + AHEAD) + 4, OUT_TILES))
+            if n < CHUNKS - 2:
+                for m in range(OUT_TILES):
+                    multiply(n, m)
 
         for m in range(OUT_TILES):
+            multiply(CHUNKS - 2, m)
+            multiply(CHUNKS - 1, m)
             nc.vector.tensor_tensor(out=rest[:, m, :], in0=acc[m][:], in1=rest[:, m, :], op=ALU.add)
             for b in range(IMAGES):
                 nc.sync.dma_start(

@@ -30,9 +30,10 @@ EARLY_TILES = 7
 EARLY_ROWS = EARLY_TILES * P // ROW_PITCH
 RUN = 16
 CHUNKS = TAPS * HALVES
+GROUP = TAPS_H * HALVES
 RAW_BUFS = 4
 AHEAD = 4
-VECTOR_EVERY = 9
+VECTOR_EVERY = 18
 FIRST_SCALE_STEP = 2
 STAGES = 4
 FLOPS = 2 * IMAGES * ROWS_OUT * COLS_OUT * TAPS * CHANNELS * 8 * FEATURES
@@ -60,26 +61,6 @@ def tile_conv2dkan_pa_kernel(tc, x, spline_kernel, scale_factor, base, kan_bias,
                 out=x_sb[b:P:IMAGES, :, :],
                 in_=x[b].rearrange("r q c -> (r q) c").rearrange("(i s) c -> s i c", s=P // IMAGES),
             )
-        factors = keep.tile([P, TAPS, FEATURES], BF16)
-        for partitions, first in channel_runs:
-            nc.sync.dma_start(
-                out=factors[partitions, :, :],
-                in_=scale_factor.rearrange("(tap c) o -> c tap o", c=CHANNELS)[first : first + RUN],
-            )
-
-        raw_of = {}
-
-        def load_weights(tap):
-            raw = raw_pool.tile([P, HALVES * PACK, FEATURES], BF16, name="raw")
-            for partitions, first in channel_runs:
-                nc.sync.dma_start(
-                    out=raw[partitions, :, :],
-                    in_=spline_kernel[tap * CHANNELS + first : tap * CHANNELS + first + RUN],
-                )
-            raw_of[tap] = raw
-
-        load_weights(0)
-        load_weights(1)
         bias_rows = keep.tile([P, FEATURES], BF16)
         nc.vector.memset(bias_rows[:], 0.0)
         nc.sync.dma_start(out=bias_rows[0:1, :], in_=kan_bias.rearrange("(a o) -> a o", a=1))
@@ -90,8 +71,30 @@ def tile_conv2dkan_pa_kernel(tc, x, spline_kernel, scale_factor, base, kan_bias,
                 out=base_sb[b:P:IMAGES, :, :],
                 in_=base[b].rearrange("p q o -> (p q) o").rearrange("(m s) o -> s m o", s=P // IMAGES),
             )
-        for tap in range(2, RAW_BUFS):
-            load_weights(tap)
+        factors = keep.tile([P, TAPS, FEATURES], BF16)
+        for partitions, first in channel_runs:
+            nc.sync.dma_start(
+                out=factors[partitions, :, :],
+                in_=scale_factor.rearrange("(tap c) o -> c tap o", c=CHANNELS)[first : first + RUN],
+            )
+
+        raw_of = {}
+
+        def tap_of(n):
+            return ((n % GROUP) // HALVES) * TAPS_W + n // GROUP
+
+        def load_weights(place):
+            tap = tap_of(place * HALVES)
+            raw = raw_pool.tile([P, HALVES * PACK, FEATURES], BF16, name="raw")
+            for partitions, first in channel_runs:
+                nc.sync.dma_start(
+                    out=raw[partitions, :, :],
+                    in_=spline_kernel[tap * CHANNELS + first : tap * CHANNELS + first + RUN],
+                )
+            raw_of[place] = raw
+
+        for place in range(RAW_BUFS):
+            load_weights(place)
 
         ident = keep.tile([P, P], BF16)
         make_identity(nc, ident[:])
@@ -137,8 +140,9 @@ def tile_conv2dkan_pa_kernel(tc, x, spline_kernel, scale_factor, base, kan_bias,
             return n % VECTOR_EVERY == VECTOR_EVERY - 1
 
         def scale_weights(n):
-            tap, half = divmod(n, HALVES)
-            rows = raw_of[tap][:, half * PACK : (half + 1) * PACK, :]
+            place, half = divmod(n, HALVES)
+            tap = tap_of(n)
+            rows = raw_of[place][:, half * PACK : (half + 1) * PACK, :]
             if by_vector(n):
                 grouped = weight_pool.tile([P, FEATURES, PACK], BF16, name="grouped", align_bytes=64)
                 nc.vector.tensor_tensor(
@@ -157,8 +161,8 @@ def tile_conv2dkan_pa_kernel(tc, x, spline_kernel, scale_factor, base, kan_bias,
                     op=ALU.mult,
                 )
                 scaled_of[n] = scaled
-            if half == HALVES - 1 and tap + RAW_BUFS < TAPS:
-                load_weights(tap + RAW_BUFS)
+            if half == HALVES - 1 and place + RAW_BUFS < TAPS:
+                load_weights(place + RAW_BUFS)
 
         def regroup_weights(n):
             if not by_vector(n):
@@ -192,18 +196,19 @@ def tile_conv2dkan_pa_kernel(tc, x, spline_kernel, scale_factor, base, kan_bias,
 
         def copy_tap(dj, first_row, end_row):
             rows = slice(first_row, end_row)
-            nc.vector.tensor_copy(
-                out=tap_codes[dj][:].bitcast(I32).rearrange("p h (r w) -> p h r w", w=ROW_WINDOW)[:, :, rows, :],
-                in_=basis_codes[:].bitcast(I32).rearrange("p h (r w) -> p h r w", w=ROW_PITCH)[
-                    :, :, rows, dj * IMAGES : dj * IMAGES + ROW_WINDOW
-                ],
-            )
-            nc.vector.tensor_copy(
-                out=tap_scales[dj][:].bitcast(I32).rearrange("p h (r w) -> p h r w", w=ROW_WINDOW // 4)[:, :, rows, :],
-                in_=basis_scales[:].bitcast(I32).rearrange("p h (r w) -> p h r w", w=ROW_PITCH // 4)[
-                    :, :, rows, dj : dj + ROW_WINDOW // 4
-                ],
-            )
+            for half in range(HALVES):
+                nc.vector.tensor_copy(
+                    out=tap_codes[dj][:, half, :].bitcast(I32).rearrange("p (r w) -> p r w", w=ROW_WINDOW)[:, rows, :],
+                    in_=basis_codes[:, half, :].bitcast(I32).rearrange("p (r w) -> p r w", w=ROW_PITCH)[
+                        :, rows, dj * IMAGES : dj * IMAGES + ROW_WINDOW
+                    ],
+                )
+                nc.vector.tensor_copy(
+                    out=tap_scales[dj][:, half, :].bitcast(I32).rearrange("p (r w) -> p r w", w=ROW_WINDOW // 4)[:, rows, :],
+                    in_=basis_scales[:, half, :].bitcast(I32).rearrange("p (r w) -> p r w", w=ROW_PITCH // 4)[
+                        :, rows, dj : dj + ROW_WINDOW // 4
+                    ],
+                )
 
         bias_psum = ctx.enter_context(tc.psum_pool(name="bias", bufs=1))
         with tc.psum_pool(name="offsets", bufs=4) as offset_psum:
@@ -299,6 +304,17 @@ def tile_conv2dkan_pa_kernel(tc, x, spline_kernel, scale_factor, base, kan_bias,
 
             offsets(0)
             offsets(1)
+            bias_ps = bias_psum.tile([P, FEATURES], F32)
+            nc.tensor.matmul(out=bias_ps[:], lhsT=ones[:], rhs=bias_rows[:], start=True, stop=True)
+
+            def add_biases(first_tile, end_tile):
+                nc.vector.tensor_tensor(
+                    out=rest[:, first_tile:end_tile, :],
+                    in0=base_sb[:, first_tile:end_tile, :],
+                    in1=bias_ps[:].unsqueeze(1).to_broadcast([P, end_tile - first_tile, FEATURES]),
+                    op=ALU.add,
+                )
+
             def live(i):
                 return 0 <= i < X_TILES
 
@@ -332,32 +348,26 @@ def tile_conv2dkan_pa_kernel(tc, x, spline_kernel, scale_factor, base, kan_bias,
                     lower_half(fourth)
                 if live(third):
                     signed(third)
+                if step < 2:
+                    add_biases(4 * step, min(4 * step + 4, OUT_TILES))
                 if fourth == EARLY_TILES - 1:
                     quantise_basis(0, (512, 256, 128))
                     copy_tap(0, 0, EARLY_ROWS)
+                    regroup_weights(0)
+                    regroup_weights(1)
+                    for n in range(HALVES):
+                        quantise_weights(n)
                 if FIRST_SCALE_STEP <= step < FIRST_SCALE_STEP + AHEAD:
                     scale_weights(step - FIRST_SCALE_STEP)
-            regroup_weights(0)
             quantise_basis(EARLY_TILES * P, (256,))
             copy_tap(0, EARLY_ROWS, ROWS_IN)
-
-        bias_ps = bias_psum.tile([P, FEATURES], F32)
-        nc.tensor.matmul(out=bias_ps[:], lhsT=ones[:], rhs=bias_rows[:], start=True, stop=True)
-
-        def add_biases(first_tile, end_tile):
-            nc.vector.tensor_tensor(
-                out=rest[:, first_tile:end_tile, :],
-                in0=base_sb[:, first_tile:end_tile, :],
-                in1=bias_ps[:].unsqueeze(1).to_broadcast([P, end_tile - first_tile, FEATURES]),
-                op=ALU.add,
-            )
 
         acc_pool = ctx.enter_context(tc.psum_pool(name="acc", bufs=1, reuse_waits="tile"))
         acc = [acc_pool.tile([P, FEATURES], F32, name="acc%d" % m) for m in range(OUT_TILES)]
 
         def multiply(n, m):
-            tap, half = divmod(n, HALVES)
-            di, dj = divmod(tap, TAPS_W)
+            half = n % HALVES
+            di, dj = divmod(tap_of(n), TAPS_W)
             window = slice((2 * m + di) * ROW_WINDOW, (2 * m + di) * ROW_WINDOW + P)
             w_codes, w_scales = codes_of[n]
             nc.tensor.matmul_mx(
@@ -371,18 +381,20 @@ def tile_conv2dkan_pa_kernel(tc, x, spline_kernel, scale_factor, base, kan_bias,
             )
 
         for n in range(CHUNKS):
-            quantise_weights(n)
-            if n + 1 < TAPS_W:
-                copy_tap(n + 1, 0, ROWS_IN)
+            if n >= HALVES:
+                quantise_weights(n)
+            if n % GROUP == GROUP // 2 and n // GROUP + 1 < TAPS_W:
+                copy_tap(n // GROUP + 1, 0, ROWS_IN)
             if n + AHEAD < CHUNKS:
                 scale_weights(n + AHEAD)
-            if n + 1 < CHUNKS:
+            if HALVES <= n + 1 < CHUNKS:
                 regroup_weights(n + 1)
-            if CHUNKS - AHEAD <= n < CHUNKS - AHEAD + 2:
-                add_biases(4 * (n - CHUNKS + AHEAD), min(4 * (n - CHUNKS + AHEAD) + 4, OUT_TILES))
-            if n < CHUNKS - 2:
-                for m in range(OUT_TILES):
+            if n < CHUNKS - HALVES:
+                for m in range(OUT_TILES - 1):
                     multiply(n, m)
+                if n % HALVES == HALVES - 1:
+                    multiply(n - 1, OUT_TILES - 1)
+                    multiply(n, OUT_TILES - 1)
 
         for m in range(OUT_TILES):
             multiply(CHUNKS - 2, m)

@@ -34,7 +34,7 @@ GROUP = TAPS_H * HALVES
 RAW_BUFS = 4
 AHEAD = 4
 VECTOR_EVERY = 18
-FIRST_SCALE_STEP = 2
+FIRST_SCALE_STEP = 4
 STAGES = 4
 FLOPS = 2 * IMAGES * ROWS_OUT * COLS_OUT * TAPS * CHANNELS * 8 * FEATURES
 

@@ -215,10 +215,10 @@ def tile_conv2dkan_pa_kernel(tc, x, spline_kernel, scale_factor, base, kan_bias,
             offset_of = {}
             dist_of = {}
             side_of = {}
+            reach_of = {}
+            square_of = {}
             outer_of = {}
             inner_of = {}
-            outer_cube_of = {}
-            inner_cube_of = {}
             value_of = {}
             signed_of = {}
 
@@ -243,58 +243,70 @@ def tile_conv2dkan_pa_kernel(tc, x, spline_kernel, scale_factor, base, kan_bias,
             def distance(i):
                 nc.scalar.activation(out=dist_of[i][:], in_=dist_of[i][:], func=ACT.Abs, bias=-2.0, scale=1.0)
 
-            def outer(i):
-                outer_of[i] = work.tile([P, TILE_VALUES], F32, name="outer")
-                nc.scalar.activation(out=outer_of[i][:], in_=dist_of[i][:], func=ACT.Relu, bias=2.0, scale=-1.0)
+            def reach(i):
+                reach_of[i] = work.tile([P, TILE_VALUES], F32, name="reach")
+                nc.scalar.activation(out=reach_of[i][:], in_=dist_of[i][:], func=ACT.Relu, bias=2.0, scale=-1.0)
 
-            def outer_square(i):
-                outer_cube_of[i] = work.tile([P, TILE_VALUES], F32, name="outer_cube")
+            def square(i):
+                square_of[i] = work.tile([P, TILE_VALUES], F32, name="square")
                 nc.scalar.activation(
-                    out=outer_cube_of[i][:], in_=outer_of[i][:], func=ACT.Square, scale=math.sqrt(1.0 / 6.0)
-                )
-
-            def inner_square(i):
-                inner_cube_of[i] = work.tile([P, TILE_VALUES], F32, name="inner_cube")
-                nc.scalar.activation(
-                    out=inner_cube_of[i][:],
+                    out=square_of[i][:],
                     in_=dist_of[i][:],
                     func=ACT.Square,
-                    bias=math.sqrt(2.0 / 3.0),
-                    scale=-math.sqrt(2.0 / 3.0),
+                    bias=2.0 * math.sqrt(0.5),
+                    scale=-math.sqrt(0.5),
                 )
+
+            def outer(i):
+                outer_of[i] = work.tile([P, TILE_VALUES], F32, name="outer")
+                nc.vector.scalar_tensor_tensor(
+                    out=outer_of[i][:],
+                    in0=reach_of[i][:],
+                    scalar=-1.0 / 3.0,
+                    in1=square_of[i][:],
+                    op0=ALU.mult,
+                    op1=ALU.mult,
+                )
+
+            def by_pairs(tile):
+                return tile[:].rearrange("p (c h t) -> p c h t", h=2, t=2)
 
             def inner(i):
                 inner_of[i] = work.tile([P, TILE_VALUES], F32, name="inner")
-                nc.vector.tensor_scalar(
-                    out=inner_of[i][:], in0=dist_of[i][:], scalar1=1.0, scalar2=1.0, op0=ALU.min, op1=ALU.subtract
+                nc.vector.tensor_tensor(
+                    out=by_pairs(inner_of[i]),
+                    in0=by_pairs(reach_of[i]),
+                    in1=by_pairs(square_of[i])[:, :, ::-1, :],
+                    op=ALU.mult,
                 )
-
-            def outer_cube(i):
-                nc.vector.tensor_tensor(out=outer_cube_of[i][:], in0=outer_cube_of[i][:], in1=outer_of[i][:], op=ALU.mult)
-
-            def inner_cube(i):
-                nc.vector.tensor_tensor(out=inner_cube_of[i][:], in0=inner_cube_of[i][:], in1=inner_of[i][:], op=ALU.mult)
 
             def value(i):
                 value_of[i] = work.tile([P, TILE_VALUES], BF16, name="value")
-                nc.vector.tensor_tensor(out=value_of[i][:], in0=outer_cube_of[i][:], in1=inner_cube_of[i][:], op=ALU.add)
+                nc.vector.scalar_tensor_tensor(
+                    out=value_of[i][:],
+                    in0=inner_of[i][:],
+                    scalar=2.0 / 3.0,
+                    in1=outer_of[i][:],
+                    op0=ALU.subtract,
+                    op1=ALU.max,
+                )
 
             def signed(i):
                 signed_of[i] = work.tile([P, TILE_VALUES], BF16, name="signed")
                 nc.vector.tensor_tensor(out=signed_of[i][:], in0=value_of[i][:], in1=side_of[i][:], op=ALU.mult)
 
-            def upper_half(i):
+            def lower_half(i):
                 nc.vector.tensor_scalar(
-                    out=basis_bf[:, 1, i * TILE_VALUES : (i + 1) * TILE_VALUES],
+                    out=basis_bf[:, 0, i * TILE_VALUES : (i + 1) * TILE_VALUES],
                     in0=signed_of[i][:],
                     scalar1=0.0,
                     scalar2=None,
                     op0=ALU.max,
                 )
 
-            def lower_half(i):
+            def upper_half(i):
                 nc.vector.tensor_scalar(
-                    out=basis_bf[:, 0, i * TILE_VALUES : (i + 1) * TILE_VALUES],
+                    out=basis_bf[:, 1, i * TILE_VALUES : (i + 1) * TILE_VALUES],
                     in0=signed_of[i][:],
                     scalar1=-1.0,
                     scalar2=0.0,
@@ -325,27 +337,23 @@ def tile_conv2dkan_pa_kernel(tc, x, spline_kernel, scale_factor, base, kan_bias,
                 if live(first):
                     fold(first)
                 if live(second):
-                    outer(second)
+                    reach(second)
                 if live(first):
                     side(first)
                 if live(second):
-                    outer_square(second)
+                    square(second)
                 if live(first):
                     distance(first)
-                if live(second):
-                    inner_square(second)
                 if live(third):
-                    outer_cube(third)
-                if live(second):
-                    inner(second)
+                    outer(third)
                 if live(third):
-                    inner_cube(third)
+                    inner(third)
                 if live(fourth):
-                    upper_half(fourth)
+                    lower_half(fourth)
                 if live(third):
                     value(third)
                 if live(fourth):
-                    lower_half(fourth)
+                    upper_half(fourth)
                 if live(third):
                     signed(third)
                 if step < 2:

@@ -28,13 +28,16 @@ TILE_VALUES = P * PACK
 OUT_TILES = ROWS_OUT // 2
 EARLY_TILES = 7
 EARLY_ROWS = EARLY_TILES * P // ROW_PITCH
-RUN = 16
+RUN = 32
 CHUNKS = TAPS * HALVES
 GROUP = TAPS_H * HALVES
 RAW_BUFS = 4
-AHEAD = 4
+AHEAD = 6
+LEAD = 5
 VECTOR_EVERY = 18
-FIRST_SCALE_STEP = 4
+HEAD_SCALES = 2
+SCALE_STEPS = (4, 6, 8, 9)
+REST_ROUNDS = (9, 12)
 STAGES = 4
 FLOPS = 2 * IMAGES * ROWS_OUT * COLS_OUT * TAPS * CHANNELS * 8 * FEATURES
 
@@ -46,7 +49,8 @@ def tile_conv2dkan_pa_kernel(tc, x, spline_kernel, scale_factor, base, kan_bias,
         keep = ctx.enter_context(tc.tile_pool(name="keep", bufs=1))
         work = ctx.enter_context(tc.tile_pool(name="work", bufs=3))
         raw_pool = ctx.enter_context(tc.tile_pool(name="raw", bufs=RAW_BUFS))
-        weight_pool = ctx.enter_context(tc.tile_pool(name="weight", bufs=AHEAD + 2))
+        scaled_pool = ctx.enter_context(tc.tile_pool(name="scaled", bufs=AHEAD + 1))
+        grouped_pool = ctx.enter_context(tc.tile_pool(name="grouped", bufs=LEAD + 1))
         code_pool = ctx.enter_context(tc.tile_pool(name="code", bufs=4))
 
         def partitions_of_run(first):
@@ -61,22 +65,18 @@ def tile_conv2dkan_pa_kernel(tc, x, spline_kernel, scale_factor, base, kan_bias,
                 out=x_sb[b:P:IMAGES, :, :],
                 in_=x[b].rearrange("r q c -> (r q) c").rearrange("(i s) c -> s i c", s=P // IMAGES),
             )
-        bias_rows = keep.tile([P, FEATURES], BF16)
-        nc.vector.memset(bias_rows[:], 0.0)
-        nc.sync.dma_start(out=bias_rows[0:1, :], in_=kan_bias.rearrange("(a o) -> a o", a=1))
-        nc.sync.dma_start(out=bias_rows[1:2, :], in_=conv_bias.rearrange("(a o) -> a o", a=1))
-        base_sb = keep.tile([P, OUT_TILES, FEATURES], BF16)
-        for b in range(IMAGES):
-            nc.sync.dma_start(
-                out=base_sb[b:P:IMAGES, :, :],
-                in_=base[b].rearrange("p q o -> (p q) o").rearrange("(m s) o -> s m o", s=P // IMAGES),
-            )
-        factors = keep.tile([P, TAPS, FEATURES], BF16)
-        for partitions, first in channel_runs:
-            nc.sync.dma_start(
-                out=factors[partitions, :, :],
-                in_=scale_factor.rearrange("(tap c) o -> c tap o", c=CHANNELS)[first : first + RUN],
-            )
+        factors_first = keep.tile([P, 1, FEATURES], BF16)
+        factors_rest = keep.tile([P, TAPS - 1, FEATURES], BF16)
+
+        def load_factors(tile, first_tap, end_tap):
+            for partitions, first in channel_runs:
+                nc.sync.dma_start(
+                    out=tile[partitions, :, :],
+                    in_=scale_factor.rearrange("(tap c) o -> c tap o", c=CHANNELS)[first : first + RUN, first_tap:end_tap, :],
+                )
+
+        def factors_of(tap):
+            return factors_first[:, 0, :] if tap == 0 else factors_rest[:, tap - 1, :]
 
         raw_of = {}
 
@@ -93,8 +93,22 @@ def tile_conv2dkan_pa_kernel(tc, x, spline_kernel, scale_factor, base, kan_bias,
                 )
             raw_of[place] = raw
 
-        for place in range(RAW_BUFS):
+        load_factors(factors_first, 0, 1)
+        load_weights(0)
+        load_factors(factors_rest, 1, TAPS)
+        load_weights(1)
+        bias_rows = keep.tile([P, FEATURES], BF16)
+        nc.vector.memset(bias_rows[:], 0.0)
+        nc.sync.dma_start(out=bias_rows[0:1, :], in_=kan_bias.rearrange("(a o) -> a o", a=1))
+        nc.sync.dma_start(out=bias_rows[1:2, :], in_=conv_bias.rearrange("(a o) -> a o", a=1))
+        for place in range(2, RAW_BUFS):
             load_weights(place)
+        base_sb = keep.tile([P, OUT_TILES, FEATURES], BF16)
+        for b in range(IMAGES):
+            nc.sync.dma_start(
+                out=base_sb[b:P:IMAGES, :, :],
+                in_=base[b].rearrange("p q o -> (p q) o").rearrange("(m s) o -> s m o", s=P // IMAGES),
+            )
 
         ident = keep.tile([P, P], BF16)
         make_identity(nc, ident[:])
@@ -144,20 +158,20 @@ def tile_conv2dkan_pa_kernel(tc, x, spline_kernel, scale_factor, base, kan_bias,
             tap = tap_of(n)
             rows = raw_of[place][:, half * PACK : (half + 1) * PACK, :]
             if by_vector(n):
-                grouped = weight_pool.tile([P, FEATURES, PACK], BF16, name="grouped", align_bytes=64)
+                grouped = grouped_pool.tile([P, FEATURES, PACK], BF16, name="grouped", align_bytes=64)
                 nc.vector.tensor_tensor(
                     out=grouped[:],
                     in0=rows.rearrange("p j o -> p o j"),
-                    in1=factors[:, tap, :].unsqueeze(2).to_broadcast([P, FEATURES, PACK]),
+                    in1=factors_of(tap).unsqueeze(2).to_broadcast([P, FEATURES, PACK]),
                     op=ALU.mult,
                 )
                 grouped_of[n] = grouped
             else:
-                scaled = weight_pool.tile([P, PACK, FEATURES], BF16, name="scaled")
+                scaled = scaled_pool.tile([P, PACK, FEATURES], BF16, name="scaled")
                 nc.vector.tensor_tensor(
                     out=scaled[:],
                     in0=rows,
-                    in1=factors[:, tap, :].unsqueeze(1).to_broadcast([P, PACK, FEATURES]),
+                    in1=factors_of(tap).unsqueeze(1).to_broadcast([P, PACK, FEATURES]),
                     op=ALU.mult,
                 )
                 scaled_of[n] = scaled
@@ -166,7 +180,7 @@ def tile_conv2dkan_pa_kernel(tc, x, spline_kernel, scale_factor, base, kan_bias,
 
         def regroup_weights(n):
             if not by_vector(n):
-                grouped = weight_pool.tile([P, FEATURES, PACK], BF16, name="grouped", align_bytes=64)
+                grouped = grouped_pool.tile([P, FEATURES, PACK], BF16, name="grouped", align_bytes=64)
                 nc.scalar.copy(
                     out=grouped[:].rearrange("p (c i) j -> p c j i", i=4),
                     in_=scaled_of[n][:].rearrange("p j (c i) -> p c j i", i=4),
@@ -194,15 +208,19 @@ def tile_conv2dkan_pa_kernel(tc, x, spline_kernel, scale_factor, base, kan_bias,
                     )
                     first = first + width
 
-        def copy_tap(dj, first_row, end_row):
+        def copy_tap_codes(dj, first_row, end_row, move):
             rows = slice(first_row, end_row)
             for half in range(HALVES):
-                nc.vector.tensor_copy(
+                move(
                     out=tap_codes[dj][:, half, :].bitcast(I32).rearrange("p (r w) -> p r w", w=ROW_WINDOW)[:, rows, :],
                     in_=basis_codes[:, half, :].bitcast(I32).rearrange("p (r w) -> p r w", w=ROW_PITCH)[
                         :, rows, dj * IMAGES : dj * IMAGES + ROW_WINDOW
                     ],
                 )
+
+        def copy_tap_scales(dj, first_row, end_row):
+            rows = slice(first_row, end_row)
+            for half in range(HALVES):
                 nc.vector.tensor_copy(
                     out=tap_scales[dj][:, half, :].bitcast(I32).rearrange("p (r w) -> p r w", w=ROW_WINDOW // 4)[:, rows, :],
                     in_=basis_scales[:, half, :].bitcast(I32).rearrange("p (r w) -> p r w", w=ROW_PITCH // 4)[
@@ -225,10 +243,10 @@ def tile_conv2dkan_pa_kernel(tc, x, spline_kernel, scale_factor, base, kan_bias,
             def offsets(i):
                 offset = offset_psum.tile([P, TILE_VALUES], F32, name="offset")
                 nc.tensor.matmul(
-                    out=offset[:], lhsT=x_sorted[:, i, :], rhs=stretch[:].rearrange("s c t -> s (c t)"), start=True, stop=False
+                    out=offset[:], lhsT=ones[:], rhs=shift[:].rearrange("s c t -> s (c t)"), start=True, stop=False
                 )
                 nc.tensor.matmul(
-                    out=offset[:], lhsT=ones[:], rhs=shift[:].rearrange("s c t -> s (c t)"), start=False, stop=True
+                    out=offset[:], lhsT=x_sorted[:, i, :], rhs=stretch[:].rearrange("s c t -> s (c t)"), start=False, stop=True
                 )
                 offset_of[i] = offset
 
@@ -317,7 +335,6 @@ def tile_conv2dkan_pa_kernel(tc, x, spline_kernel, scale_factor, base, kan_bias,
             offsets(0)
             offsets(1)
             bias_ps = bias_psum.tile([P, FEATURES], F32)
-            nc.tensor.matmul(out=bias_ps[:], lhsT=ones[:], rhs=bias_rows[:], start=True, stop=True)
 
             def add_biases(first_tile, end_tile):
                 nc.vector.tensor_tensor(
@@ -327,6 +344,8 @@ def tile_conv2dkan_pa_kernel(tc, x, spline_kernel, scale_factor, base, kan_bias,
                     op=ALU.add,
                 )
 
+            for n in range(HEAD_SCALES):
+                scale_weights(n)
             def live(i):
                 return 0 <= i < X_TILES
 
@@ -356,19 +375,23 @@ def tile_conv2dkan_pa_kernel(tc, x, spline_kernel, scale_factor, base, kan_bias,
                     upper_half(fourth)
                 if live(third):
                     signed(third)
-                if step < 2:
-                    add_biases(4 * step, min(4 * step + 4, OUT_TILES))
                 if fourth == EARLY_TILES - 1:
                     quantise_basis(0, (512, 256, 128))
-                    copy_tap(0, 0, EARLY_ROWS)
-                    regroup_weights(0)
-                    regroup_weights(1)
+                    copy_tap_codes(0, 0, EARLY_ROWS, nc.vector.tensor_copy)
+                    copy_tap_scales(0, 0, EARLY_ROWS)
+                    for n in range(LEAD - 1):
+                        regroup_weights(n)
                     for n in range(HALVES):
                         quantise_weights(n)
-                if FIRST_SCALE_STEP <= step < FIRST_SCALE_STEP + AHEAD:
-                    scale_weights(step - FIRST_SCALE_STEP)
+                if step in SCALE_STEPS:
+                    scale_weights(HEAD_SCALES + SCALE_STEPS.index(step))
+            nc.tensor.matmul(out=bias_ps[:], lhsT=ones[:], rhs=bias_rows[:], start=True, stop=True)
+            regroup_weights(LEAD - 1)
             quantise_basis(EARLY_TILES * P, (256,))
-            copy_tap(0, EARLY_ROWS, ROWS_IN)
+            copy_tap_codes(0, EARLY_ROWS, ROWS_IN, nc.vector.tensor_copy)
+            copy_tap_scales(0, EARLY_ROWS, ROWS_IN)
+            for dj in range(1, TAPS_W):
+                copy_tap_codes(dj, 0, ROWS_IN, nc.sync.dma_start)
 
         acc_pool = ctx.enter_context(tc.psum_pool(name="acc", bufs=1, reuse_waits="tile"))
         acc = [acc_pool.tile([P, FEATURES], F32, name="acc%d" % m) for m in range(OUT_TILES)]
@@ -392,11 +415,14 @@ def tile_conv2dkan_pa_kernel(tc, x, spline_kernel, scale_factor, base, kan_bias,
             if n >= HALVES:
                 quantise_weights(n)
             if n % GROUP == GROUP // 2 and n // GROUP + 1 < TAPS_W:
-                copy_tap(n // GROUP + 1, 0, ROWS_IN)
+                copy_tap_scales(n // GROUP + 1, 0, ROWS_IN)
             if n + AHEAD < CHUNKS:
                 scale_weights(n + AHEAD)
-            if HALVES <= n + 1 < CHUNKS:
-                regroup_weights(n + 1)
+            if n in REST_ROUNDS:
+                first_tile = 4 * REST_ROUNDS.index(n)
+                add_biases(first_tile, min(first_tile + 4, OUT_TILES))
+            if n + LEAD < CHUNKS:
+                regroup_weights(n + LEAD)
             if n < CHUNKS - HALVES:
                 for m in range(OUT_TILES - 1):
                     multiply(n, m)

@@ -32,12 +32,12 @@ RUN = 32
 CHUNKS = TAPS * HALVES
 GROUP = TAPS_H * HALVES
 RAW_BUFS = 4
-AHEAD = 6
-LEAD = 5
-VECTOR_EVERY = 18
+AHEAD = 4
+LEAD = 3
+VECTOR_EVERY = 6
 HEAD_SCALES = 2
-SCALE_STEPS = (4, 6, 8, 9)
-REST_ROUNDS = (9, 12)
+FIRST_REST_STEP = 4
+SCALE_STEPS = (5, 8)
 STAGES = 4
 FLOPS = 2 * IMAGES * ROWS_OUT * COLS_OUT * TAPS * CHANNELS * 8 * FEATURES
 
@@ -57,7 +57,15 @@ def tile_conv2dkan_pa_kernel(tc, x, spline_kernel, scale_factor, base, kan_bias,
             a, b = divmod(first // RUN, 2)
             return slice(2 * RUN * a + b, 2 * RUN * (a + 1), 2)
 
+        def queue_of(first, tap):
+            if first < CHANNELS // 2:
+                return nc.sync
+            return nc.scalar if tap == 0 else nc.gpsimd
+
         channel_runs = [(partitions_of_run(first), first) for first in range(0, CHANNELS, RUN)]
+
+        ident = keep.tile([P, P], BF16)
+        make_identity(nc, ident[:])
 
         x_sb = keep.tile([P, X_TILES, CHANNELS], BF16)
         for b in range(IMAGES):
@@ -70,7 +78,7 @@ def tile_conv2dkan_pa_kernel(tc, x, spline_kernel, scale_factor, base, kan_bias,
 
         def load_factors(tile, first_tap, end_tap):
             for partitions, first in channel_runs:
-                nc.sync.dma_start(
+                queue_of(first, first_tap).dma_start(
                     out=tile[partitions, :, :],
                     in_=scale_factor.rearrange("(tap c) o -> c tap o", c=CHANNELS)[first : first + RUN, first_tap:end_tap, :],
                 )
@@ -87,7 +95,7 @@ def tile_conv2dkan_pa_kernel(tc, x, spline_kernel, scale_factor, base, kan_bias,
             tap = tap_of(place * HALVES)
             raw = raw_pool.tile([P, HALVES * PACK, FEATURES], BF16, name="raw")
             for partitions, first in channel_runs:
-                nc.sync.dma_start(
+                queue_of(first, tap).dma_start(
                     out=raw[partitions, :, :],
                     in_=spline_kernel[tap * CHANNELS + first : tap * CHANNELS + first + RUN],
                 )
@@ -101,8 +109,6 @@ def tile_conv2dkan_pa_kernel(tc, x, spline_kernel, scale_factor, base, kan_bias,
         nc.vector.memset(bias_rows[:], 0.0)
         nc.sync.dma_start(out=bias_rows[0:1, :], in_=kan_bias.rearrange("(a o) -> a o", a=1))
         nc.sync.dma_start(out=bias_rows[1:2, :], in_=conv_bias.rearrange("(a o) -> a o", a=1))
-        for place in range(2, RAW_BUFS):
-            load_weights(place)
         base_sb = keep.tile([P, OUT_TILES, FEATURES], BF16)
         for b in range(IMAGES):
             nc.sync.dma_start(
@@ -110,8 +116,9 @@ def tile_conv2dkan_pa_kernel(tc, x, spline_kernel, scale_factor, base, kan_bias,
                 in_=base[b].rearrange("p q o -> (p q) o").rearrange("(m s) o -> s m o", s=P // IMAGES),
             )
 
-        ident = keep.tile([P, P], BF16)
-        make_identity(nc, ident[:])
+        for place in range(2, RAW_BUFS):
+            load_weights(place)
+
         ones = keep.tile([P, P], BF16)
         nc.vector.memset(ones[:], 1.0)
         stretch = keep.tile([P, P, PACK], BF16)
@@ -228,8 +235,7 @@ def tile_conv2dkan_pa_kernel(tc, x, spline_kernel, scale_factor, base, kan_bias,
                     ],
                 )
 
-        bias_psum = ctx.enter_context(tc.psum_pool(name="bias", bufs=1))
-        with tc.psum_pool(name="offsets", bufs=4) as offset_psum:
+        with tc.psum_pool(name="offsets", bufs=4) as offset_psum, tc.psum_pool(name="rest", bufs=2) as rest_psum:
             offset_of = {}
             dist_of = {}
             side_of = {}
@@ -334,15 +340,12 @@ def tile_conv2dkan_pa_kernel(tc, x, spline_kernel, scale_factor, base, kan_bias,
 
             offsets(0)
             offsets(1)
-            bias_ps = bias_psum.tile([P, FEATURES], F32)
 
-            def add_biases(first_tile, end_tile):
-                nc.vector.tensor_tensor(
-                    out=rest[:, first_tile:end_tile, :],
-                    in0=base_sb[:, first_tile:end_tile, :],
-                    in1=bias_ps[:].unsqueeze(1).to_broadcast([P, end_tile - first_tile, FEATURES]),
-                    op=ALU.add,
-                )
+            def add_biases(m):
+                total = rest_psum.tile([P, FEATURES], F32, name="total")
+                nc.tensor.matmul(out=total[:], lhsT=ident[:], rhs=base_sb[:, m, :], start=True, stop=False)
+                nc.tensor.matmul(out=total[:], lhsT=ones[:], rhs=bias_rows[:], start=False, stop=True)
+                nc.scalar.copy(out=rest[:, m, :], in_=total[:])
 
             for n in range(HEAD_SCALES):
                 scale_weights(n)
@@ -379,14 +382,16 @@ def tile_conv2dkan_pa_kernel(tc, x, spline_kernel, scale_factor, base, kan_bias,
                     quantise_basis(0, (512, 256, 128))
                     copy_tap_codes(0, 0, EARLY_ROWS, nc.vector.tensor_copy)
                     copy_tap_scales(0, 0, EARLY_ROWS)
-                    for n in range(LEAD - 1):
+                    for n in range(HALVES):
                         regroup_weights(n)
                     for n in range(HALVES):
                         quantise_weights(n)
+                if 0 <= step - FIRST_REST_STEP < OUT_TILES:
+                    add_biases(step - FIRST_REST_STEP)
                 if step in SCALE_STEPS:
                     scale_weights(HEAD_SCALES + SCALE_STEPS.index(step))
-            nc.tensor.matmul(out=bias_ps[:], lhsT=ones[:], rhs=bias_rows[:], start=True, stop=True)
-            regroup_weights(LEAD - 1)
+            for n in range(HALVES, LEAD):
+                regroup_weights(n)
             quantise_basis(EARLY_TILES * P, (256,))
             copy_tap_codes(0, EARLY_ROWS, ROWS_IN, nc.vector.tensor_copy)
             copy_tap_scales(0, EARLY_ROWS, ROWS_IN)
@@ -418,9 +423,6 @@ def tile_conv2dkan_pa_kernel(tc, x, spline_kernel, scale_factor, base, kan_bias,
                 copy_tap_scales(n // GROUP + 1, 0, ROWS_IN)
             if n + AHEAD < CHUNKS:
                 scale_weights(n + AHEAD)
-            if n in REST_ROUNDS:
-                first_tile = 4 * REST_ROUNDS.index(n)
-                add_biases(first_tile, min(first_tile + 4, OUT_TILES))
             if n + LEAD < CHUNKS:
                 regroup_weights(n + LEAD)
             if n < CHUNKS - HALVES:

@@ -21,23 +21,27 @@ TAPS_H, TAPS_W = 3, 3
 TAPS = TAPS_H * TAPS_W
 HALVES = 2
 COLUMNS = ROWS_IN * COLS_IN * IMAGES
-ROW_PITCH = COLS_IN * IMAGES
 ROW_WINDOW = COLS_OUT * IMAGES
+MAIN = ROWS_IN * ROW_WINDOW
+EDGE_PIXELS = COLS_IN - COLS_OUT
+EDGE_WIDTH = EDGE_PIXELS * IMAGES
 X_TILES = COLUMNS // P
+MAIN_TILES = MAIN // P
 TILE_VALUES = P * PACK
 OUT_TILES = ROWS_OUT // 2
-EARLY_TILES = 7
-EARLY_ROWS = EARLY_TILES * P // ROW_PITCH
+EARLY_TILES = 6
+EARLY_OUT = EARLY_TILES - 1
 RUN = 32
 CHUNKS = TAPS * HALVES
 GROUP = TAPS_H * HALVES
 RAW_BUFS = 4
 AHEAD = 4
 LEAD = 3
-VECTOR_EVERY = 6
+VECTOR_EVERY = 9
 HEAD_SCALES = 2
-FIRST_REST_STEP = 4
-SCALE_STEPS = (5, 8)
+EARLY_REST = 2
+EDGE_SORT_STEP = 3
+SCALE_STEPS = (5, 7)
 STAGES = 4
 FLOPS = 2 * IMAGES * ROWS_OUT * COLS_OUT * TAPS * CHANNELS * 8 * FEATURES
 
@@ -58,9 +62,7 @@ def tile_conv2dkan_pa_kernel(tc, x, spline_kernel, scale_factor, base, kan_bias,
             return slice(2 * RUN * a + b, 2 * RUN * (a + 1), 2)
 
         def queue_of(first, tap):
-            if first < CHANNELS // 2:
-                return nc.sync
-            return nc.scalar if tap == 0 else nc.gpsimd
+            return nc.scalar if tap == 0 and first >= CHANNELS // 2 else nc.sync
 
         channel_runs = [(partitions_of_run(first), first) for first in range(0, CHANNELS, RUN)]
 
@@ -69,10 +71,11 @@ def tile_conv2dkan_pa_kernel(tc, x, spline_kernel, scale_factor, base, kan_bias,
 
         x_sb = keep.tile([P, X_TILES, CHANNELS], BF16)
         for b in range(IMAGES):
-            nc.sync.dma_start(
-                out=x_sb[b:P:IMAGES, :, :],
-                in_=x[b].rearrange("r q c -> (r q) c").rearrange("(i s) c -> s i c", s=P // IMAGES),
-            )
+            for r in range(2):
+                (nc.sync if r == 0 else nc.scalar).dma_start(
+                    out=x_sb[r * ROW_WINDOW + b : (r + 1) * ROW_WINDOW : IMAGES, 0:MAIN_TILES, :],
+                    in_=x[b].rearrange("(i r) q c -> r q i c", r=2)[r, 0:COLS_OUT],
+                )
         factors_first = keep.tile([P, 1, FEATURES], BF16)
         factors_rest = keep.tile([P, TAPS - 1, FEATURES], BF16)
 
@@ -105,6 +108,9 @@ def tile_conv2dkan_pa_kernel(tc, x, spline_kernel, scale_factor, base, kan_bias,
         load_weights(0)
         load_factors(factors_rest, 1, TAPS)
         load_weights(1)
+        for b in range(IMAGES):
+            for e in range(EDGE_PIXELS):
+                nc.sync.dma_start(out=x_sb[e * IMAGES + b : P : EDGE_WIDTH, MAIN_TILES, :], in_=x[b, :, COLS_OUT + e, :])
         bias_rows = keep.tile([P, FEATURES], BF16)
         nc.vector.memset(bias_rows[:], 0.0)
         nc.sync.dma_start(out=bias_rows[0:1, :], in_=kan_bias.rearrange("(a o) -> a o", a=1))
@@ -133,25 +139,27 @@ def tile_conv2dkan_pa_kernel(tc, x, spline_kernel, scale_factor, base, kan_bias,
         basis_codes = keep.tile([P, HALVES, COLUMNS], U32, align_bytes=64)
         basis_scales = keep.tile([P, HALVES, COLUMNS], U8, align_bytes=64)
         nc.vector.memset(basis_scales[:].bitcast(I32), 0)
-        tap_codes = [
-            keep.tile([P, HALVES, ROWS_IN * ROW_WINDOW], U32, name="tap_codes%d" % dj, align_bytes=64)
-            for dj in range(TAPS_W)
-        ]
-        tap_scales = [
-            keep.tile([P, HALVES, ROWS_IN * ROW_WINDOW], U8, name="tap_scales%d" % dj, align_bytes=64)
-            for dj in range(TAPS_W)
-        ]
+        tap_codes = {
+            dj: keep.tile([P, HALVES, MAIN], U32, name="tap_codes%d" % dj, align_bytes=64) for dj in range(1, TAPS_W)
+        }
+        tap_scales = {
+            dj: keep.tile([P, HALVES, MAIN], U8, name="tap_scales%d" % dj, align_bytes=64) for dj in range(1, TAPS_W)
+        }
         rest = keep.tile([P, OUT_TILES, FEATURES], F32)
 
         x_sorted = keep.tile([P, X_TILES, CHANNELS], BF16)
-        nc.vector.tensor_scalar(
-            out=x_sorted[:].rearrange("s i (a c b) -> s (i a) c b", c=RUN, b=2),
-            in0=x_sb[:].rearrange("s i (a b c) -> s (i a) c b", b=2, c=RUN),
-            scalar1=-4.0,
-            scalar2=4.0,
-            op0=ALU.max,
-            op1=ALU.min,
-        )
+
+        def sort_x(first_tile, end_tile):
+            nc.vector.tensor_scalar(
+                out=x_sorted[:, first_tile:end_tile, :].rearrange("s i (a c b) -> s (i a) c b", c=RUN, b=2),
+                in0=x_sb[:, first_tile:end_tile, :].rearrange("s i (a b c) -> s (i a) c b", b=2, c=RUN),
+                scalar1=-4.0,
+                scalar2=4.0,
+                op0=ALU.max,
+                op1=ALU.min,
+            )
+
+        sort_x(0, MAIN_TILES)
 
         scaled_of = {}
         grouped_of = {}
@@ -215,27 +223,33 @@ def tile_conv2dkan_pa_kernel(tc, x, spline_kernel, scale_factor, base, kan_bias,
                     )
                     first = first + width
 
-        def copy_tap_codes(dj, first_row, end_row, move):
-            rows = slice(first_row, end_row)
-            for half in range(HALVES):
-                move(
-                    out=tap_codes[dj][:, half, :].bitcast(I32).rearrange("p (r w) -> p r w", w=ROW_WINDOW)[:, rows, :],
-                    in_=basis_codes[:, half, :].bitcast(I32).rearrange("p (r w) -> p r w", w=ROW_PITCH)[
-                        :, rows, dj * IMAGES : dj * IMAGES + ROW_WINDOW
-                    ],
-                )
+        def rows_of(tile, first, end):
+            return tile[:, :, first:end].bitcast(I32).rearrange("p h (r w) -> p h r w", r=ROWS_IN)
 
-        def copy_tap_scales(dj, first_row, end_row):
-            rows = slice(first_row, end_row)
-            for half in range(HALVES):
-                nc.vector.tensor_copy(
-                    out=tap_scales[dj][:, half, :].bitcast(I32).rearrange("p (r w) -> p r w", w=ROW_WINDOW // 4)[:, rows, :],
-                    in_=basis_scales[:, half, :].bitcast(I32).rearrange("p (r w) -> p r w", w=ROW_PITCH // 4)[
-                        :, rows, dj : dj + ROW_WINDOW // 4
-                    ],
-                )
+        def shift_tap(dj):
+            shift_by = dj * IMAGES
+            nc.sync.dma_start(
+                out=tap_codes[dj][:, :, 0 : MAIN - shift_by].bitcast(I32),
+                in_=basis_codes[:, :, shift_by:MAIN].bitcast(I32),
+            )
+            nc.sync.dma_start(
+                out=tap_scales[dj][:, :, 0 : MAIN - shift_by].bitcast(I32),
+                in_=basis_scales[:, :, shift_by:MAIN].bitcast(I32),
+            )
 
-        with tc.psum_pool(name="offsets", bufs=4) as offset_psum, tc.psum_pool(name="rest", bufs=2) as rest_psum:
+        def mend_tap(dj):
+            stay = COLS_OUT - dj
+            nc.vector.tensor_copy(
+                out=rows_of(tap_codes[dj], 0, MAIN)[:, :, :, stay * IMAGES : ROW_WINDOW],
+                in_=rows_of(basis_codes, MAIN, COLUMNS)[:, :, :, 0 : dj * IMAGES],
+            )
+            nc.vector.tensor_copy(
+                out=rows_of(tap_scales[dj], 0, MAIN)[:, :, :, stay:COLS_OUT],
+                in_=rows_of(basis_scales, MAIN, COLUMNS)[:, :, :, 0:dj],
+            )
+
+        rest_psum = ctx.enter_context(tc.psum_pool(name="rest", bufs=1))
+        with tc.psum_pool(name="offsets", bufs=4) as offset_psum:
             offset_of = {}
             dist_of = {}
             side_of = {}
@@ -379,24 +393,25 @@ def tile_conv2dkan_pa_kernel(tc, x, spline_kernel, scale_factor, base, kan_bias,
                 if live(third):
                     signed(third)
                 if fourth == EARLY_TILES - 1:
-                    quantise_basis(0, (512, 256, 128))
-                    copy_tap_codes(0, 0, EARLY_ROWS, nc.vector.tensor_copy)
-                    copy_tap_scales(0, 0, EARLY_ROWS)
+                    quantise_basis(0, (512, 256))
+                if step == X_TILES:
                     for n in range(HALVES):
                         regroup_weights(n)
                     for n in range(HALVES):
                         quantise_weights(n)
-                if 0 <= step - FIRST_REST_STEP < OUT_TILES:
-                    add_biases(step - FIRST_REST_STEP)
+                if fourth == MAIN_TILES - 1:
+                    quantise_basis(EARLY_TILES * P, (256,))
+                    for dj in range(1, TAPS_W):
+                        shift_tap(dj)
+                if step == EDGE_SORT_STEP:
+                    sort_x(MAIN_TILES, X_TILES)
                 if step in SCALE_STEPS:
                     scale_weights(HEAD_SCALES + SCALE_STEPS.index(step))
+            for m in range(EARLY_REST):
+                add_biases(m)
             for n in range(HALVES, LEAD):
                 regroup_weights(n)
-            quantise_basis(EARLY_TILES * P, (256,))
-            copy_tap_codes(0, EARLY_ROWS, ROWS_IN, nc.vector.tensor_copy)
-            copy_tap_scales(0, EARLY_ROWS, ROWS_IN)
-            for dj in range(1, TAPS_W):
-                copy_tap_codes(dj, 0, ROWS_IN, nc.sync.dma_start)
+            quantise_basis(MAIN, (128,))
 
         acc_pool = ctx.enter_context(tc.psum_pool(name="acc", bufs=1, reuse_waits="tile"))
         acc = [acc_pool.tile([P, FEATURES], F32, name="acc%d" % m) for m in range(OUT_TILES)]
@@ -404,12 +419,13 @@ def tile_conv2dkan_pa_kernel(tc, x, spline_kernel, scale_factor, base, kan_bias,
         def multiply(n, m):
             half = n % HALVES
             di, dj = divmod(tap_of(n), TAPS_W)
+            codes, scales = (tap_codes[dj], tap_scales[dj]) if dj > 0 else (basis_codes, basis_scales)
             window = slice((2 * m + di) * ROW_WINDOW, (2 * m + di) * ROW_WINDOW + P)
             w_codes, w_scales = codes_of[n]
             nc.tensor.matmul_mx(
                 out=acc[m][:],
-                lhsT=tap_codes[dj][:, half, window].bitcast(FP8X4),
-                lhsT_scale=tap_scales[dj][:, half, window],
+                lhsT=codes[:, half, window].bitcast(FP8X4),
+                lhsT_scale=scales[:, half, window],
                 rhs=w_codes[:].bitcast(FP8X4),
                 rhs_scale=w_scales[:],
                 start=(n == 0),
@@ -420,17 +436,23 @@ def tile_conv2dkan_pa_kernel(tc, x, spline_kernel, scale_factor, base, kan_bias,
             if n >= HALVES:
                 quantise_weights(n)
             if n % GROUP == GROUP // 2 and n // GROUP + 1 < TAPS_W:
-                copy_tap_scales(n // GROUP + 1, 0, ROWS_IN)
+                mend_tap(n // GROUP + 1)
             if n + AHEAD < CHUNKS:
                 scale_weights(n + AHEAD)
+            if 1 <= n <= OUT_TILES - EARLY_REST:
+                add_biases(EARLY_REST + n - 1)
             if n + LEAD < CHUNKS:
                 regroup_weights(n + LEAD)
-            if n < CHUNKS - HALVES:
-                for m in range(OUT_TILES - 1):
+            if n == HALVES - 1:
+                for early in range(HALVES):
+                    for m in range(EARLY_OUT):
+                        multiply(early, m)
+                for early in range(HALVES):
+                    for m in range(EARLY_OUT, OUT_TILES):
+                        multiply(early, m)
+            elif HALVES <= n < CHUNKS - HALVES:
+                for m in range(OUT_TILES):
                     multiply(n, m)
-                if n % HALVES == HALVES - 1:
-                    multiply(n - 1, OUT_TILES - 1)
-                    multiply(n, OUT_TILES - 1)
 
         for m in range(OUT_TILES):
             multiply(CHUNKS - 2, m)

@@ -20,6 +20,8 @@ ROWS_OUT, COLS_OUT, FEATURES = 14, 16, 512
 TAPS_H, TAPS_W = 3, 3
 TAPS = TAPS_H * TAPS_W
 HALVES = 2
+PASS_CHANNELS = CHANNELS // HALVES
+WORDS = 2
 COLUMNS = ROWS_IN * COLS_IN * IMAGES
 ROW_WINDOW = COLS_OUT * IMAGES
 MAIN = ROWS_IN * ROW_WINDOW
@@ -31,18 +33,17 @@ TILE_VALUES = P * PACK
 OUT_TILES = ROWS_OUT // 2
 EARLY_TILES = 6
 EARLY_OUT = EARLY_TILES - 1
-RUN = 32
 CHUNKS = TAPS * HALVES
 GROUP = TAPS_H * HALVES
-RAW_BUFS = 4
+RAW_BUFS = 8
 AHEAD = 4
 LEAD = 3
 VECTOR_EVERY = 9
 HEAD_SCALES = 2
-EARLY_REST = 2
-EDGE_SORT_STEP = 3
-SCALE_STEPS = (5, 7)
-STAGES = 4
+EARLY_REST = 1
+EDGE_CLAMP_STEP = 4
+SCALE_STEPS = (3, 4)
+STAGES = 5
 FLOPS = 2 * IMAGES * ROWS_OUT * COLS_OUT * TAPS * CHANNELS * 8 * FEATURES
 
 
@@ -52,19 +53,11 @@ def tile_conv2dkan_pa_kernel(tc, x, spline_kernel, scale_factor, base, kan_bias,
         ctx.enter_context(tc.manual_schedule())
         keep = ctx.enter_context(tc.tile_pool(name="keep", bufs=1))
         work = ctx.enter_context(tc.tile_pool(name="work", bufs=3))
+        side_pool = ctx.enter_context(tc.tile_pool(name="side", bufs=4))
         raw_pool = ctx.enter_context(tc.tile_pool(name="raw", bufs=RAW_BUFS))
         scaled_pool = ctx.enter_context(tc.tile_pool(name="scaled", bufs=AHEAD + 1))
         grouped_pool = ctx.enter_context(tc.tile_pool(name="grouped", bufs=LEAD + 1))
         code_pool = ctx.enter_context(tc.tile_pool(name="code", bufs=4))
-
-        def partitions_of_run(first):
-            a, b = divmod(first // RUN, 2)
-            return slice(2 * RUN * a + b, 2 * RUN * (a + 1), 2)
-
-        def queue_of(first, tap):
-            return nc.scalar if tap == 0 and first >= CHANNELS // 2 else nc.sync
-
-        channel_runs = [(partitions_of_run(first), first) for first in range(0, CHANNELS, RUN)]
 
         ident = keep.tile([P, P], BF16)
         make_identity(nc, ident[:])
@@ -76,38 +69,40 @@ def tile_conv2dkan_pa_kernel(tc, x, spline_kernel, scale_factor, base, kan_bias,
                     out=x_sb[r * ROW_WINDOW + b : (r + 1) * ROW_WINDOW : IMAGES, 0:MAIN_TILES, :],
                     in_=x[b].rearrange("(i r) q c -> r q i c", r=2)[r, 0:COLS_OUT],
                 )
-        factors_first = keep.tile([P, 1, FEATURES], BF16)
-        factors_rest = keep.tile([P, TAPS - 1, FEATURES], BF16)
+        factors_first = keep.tile([P, HALVES, 1, FEATURES], BF16)
+        factors_rest = keep.tile([P, HALVES, TAPS - 1, FEATURES], BF16)
 
         def load_factors(tile, first_tap, end_tap):
-            for partitions, first in channel_runs:
-                queue_of(first, first_tap).dma_start(
-                    out=tile[partitions, :, :],
-                    in_=scale_factor.rearrange("(tap c) o -> c tap o", c=CHANNELS)[first : first + RUN, first_tap:end_tap, :],
-                )
+            rows = scale_factor.rearrange("(tap c) o -> c tap o", c=CHANNELS)
+            for half in range(HALVES):
+                for h in range(WORDS):
+                    nc.sync.dma_start(
+                        out=tile[h:P:WORDS, half, :, :],
+                        in_=rows[half * PASS_CHANNELS : (half + 1) * PASS_CHANNELS, first_tap:end_tap, :],
+                    )
 
-        def factors_of(tap):
-            return factors_first[:, 0, :] if tap == 0 else factors_rest[:, tap - 1, :]
+        def factors_of(n):
+            tap = tap_of(n)
+            return factors_first[:, n % HALVES, 0, :] if tap == 0 else factors_rest[:, n % HALVES, tap - 1, :]
 
         raw_of = {}
 
         def tap_of(n):
             return ((n % GROUP) // HALVES) * TAPS_W + n // GROUP
 
-        def load_weights(place):
-            tap = tap_of(place * HALVES)
-            raw = raw_pool.tile([P, HALVES * PACK, FEATURES], BF16, name="raw")
-            for partitions, first in channel_runs:
-                queue_of(first, tap).dma_start(
-                    out=raw[partitions, :, :],
-                    in_=spline_kernel[tap * CHANNELS + first : tap * CHANNELS + first + RUN],
-                )
-            raw_of[place] = raw
+        def load_weights(n):
+            first = tap_of(n) * CHANNELS + n % HALVES * PASS_CHANNELS
+            raw_of[n] = raw_pool.tile([P, PACK, FEATURES], BF16, name="raw")
+            nc.sync.dma_start(
+                out=raw_of[n][:], in_=spline_kernel[first : first + PASS_CHANNELS].rearrange("c (h t) o -> (c h) t o", h=WORDS)
+            )
 
         load_factors(factors_first, 0, 1)
-        load_weights(0)
+        for n in range(HALVES):
+            load_weights(n)
         load_factors(factors_rest, 1, TAPS)
-        load_weights(1)
+        for n in range(HALVES, 2 * HALVES):
+            load_weights(n)
         for b in range(IMAGES):
             for e in range(EDGE_PIXELS):
                 nc.sync.dma_start(out=x_sb[e * IMAGES + b : P : EDGE_WIDTH, MAIN_TILES, :], in_=x[b, :, COLS_OUT + e, :])
@@ -122,8 +117,8 @@ def tile_conv2dkan_pa_kernel(tc, x, spline_kernel, scale_factor, base, kan_bias,
                 in_=base[b].rearrange("p q o -> (p q) o").rearrange("(m s) o -> s m o", s=P // IMAGES),
             )
 
-        for place in range(2, RAW_BUFS):
-            load_weights(place)
+        for n in range(2 * HALVES, RAW_BUFS):
+            load_weights(n)
 
         ones = keep.tile([P, P], BF16)
         nc.vector.memset(ones[:], 1.0)
@@ -147,19 +142,28 @@ def tile_conv2dkan_pa_kernel(tc, x, spline_kernel, scale_factor, base, kan_bias,
         }
         rest = keep.tile([P, OUT_TILES, FEATURES], F32)
 
-        x_sorted = keep.tile([P, X_TILES, CHANNELS], BF16)
+        x_clamped = keep.tile([P, X_TILES, CHANNELS], BF16)
 
-        def sort_x(first_tile, end_tile):
+        def clamp_x(first_tile, end_tile):
             nc.vector.tensor_scalar(
-                out=x_sorted[:, first_tile:end_tile, :].rearrange("s i (a c b) -> s (i a) c b", c=RUN, b=2),
-                in0=x_sb[:, first_tile:end_tile, :].rearrange("s i (a b c) -> s (i a) c b", b=2, c=RUN),
+                out=x_clamped[:, first_tile:end_tile, :],
+                in0=x_sb[:, first_tile:end_tile, :],
                 scalar1=-4.0,
                 scalar2=4.0,
                 op0=ALU.max,
                 op1=ALU.min,
             )
 
-        sort_x(0, MAIN_TILES)
+        clamp_x(0, MAIN_TILES)
+        spread = keep.tile([P, HALVES, PASS_CHANNELS, WORDS], BF16)
+        for h in range(WORDS):
+            nc.vector.tensor_scalar(
+                out=spread[:, :, :, h],
+                in0=ident[:].rearrange("c (half j) -> c half j", half=HALVES),
+                scalar1=1.0 - 2.0 * h,
+                scalar2=None,
+                op0=ALU.mult,
+            )
 
         scaled_of = {}
         grouped_of = {}
@@ -169,15 +173,12 @@ def tile_conv2dkan_pa_kernel(tc, x, spline_kernel, scale_factor, base, kan_bias,
             return n % VECTOR_EVERY == VECTOR_EVERY - 1
 
         def scale_weights(n):
-            place, half = divmod(n, HALVES)
-            tap = tap_of(n)
-            rows = raw_of[place][:, half * PACK : (half + 1) * PACK, :]
             if by_vector(n):
                 grouped = grouped_pool.tile([P, FEATURES, PACK], BF16, name="grouped", align_bytes=64)
                 nc.vector.tensor_tensor(
                     out=grouped[:],
-                    in0=rows.rearrange("p j o -> p o j"),
-                    in1=factors_of(tap).unsqueeze(2).to_broadcast([P, FEATURES, PACK]),
+                    in0=raw_of[n][:].rearrange("p j o -> p o j"),
+                    in1=factors_of(n).unsqueeze(2).to_broadcast([P, FEATURES, PACK]),
                     op=ALU.mult,
                 )
                 grouped_of[n] = grouped
@@ -185,13 +186,13 @@ def tile_conv2dkan_pa_kernel(tc, x, spline_kernel, scale_factor, base, kan_bias,
                 scaled = scaled_pool.tile([P, PACK, FEATURES], BF16, name="scaled")
                 nc.vector.tensor_tensor(
                     out=scaled[:],
-                    in0=rows,
-                    in1=factors_of(tap).unsqueeze(1).to_broadcast([P, PACK, FEATURES]),
+                    in0=raw_of[n][:],
+                    in1=factors_of(n).unsqueeze(1).to_broadcast([P, PACK, FEATURES]),
                     op=ALU.mult,
                 )
                 scaled_of[n] = scaled
-            if half == HALVES - 1 and place + RAW_BUFS < TAPS:
-                load_weights(place + RAW_BUFS)
+            if n + RAW_BUFS < CHUNKS:
+                load_weights(n + RAW_BUFS)
 
         def regroup_weights(n):
             if not by_vector(n):
@@ -249,7 +250,7 @@ def tile_conv2dkan_pa_kernel(tc, x, spline_kernel, scale_factor, base, kan_bias,
             )
 
         rest_psum = ctx.enter_context(tc.psum_pool(name="rest", bufs=1))
-        with tc.psum_pool(name="offsets", bufs=4) as offset_psum:
+        with tc.psum_pool(name="offsets", bufs=4) as offset_psum, tc.psum_pool(name="spread", bufs=2) as spread_psum:
             offset_of = {}
             dist_of = {}
             side_of = {}
@@ -259,6 +260,7 @@ def tile_conv2dkan_pa_kernel(tc, x, spline_kernel, scale_factor, base, kan_bias,
             inner_of = {}
             value_of = {}
             signed_of = {}
+            spread_of = {}
 
             def offsets(i):
                 offset = offset_psum.tile([P, TILE_VALUES], F32, name="offset")
@@ -266,7 +268,7 @@ def tile_conv2dkan_pa_kernel(tc, x, spline_kernel, scale_factor, base, kan_bias,
                     out=offset[:], lhsT=ones[:], rhs=shift[:].rearrange("s c t -> s (c t)"), start=True, stop=False
                 )
                 nc.tensor.matmul(
-                    out=offset[:], lhsT=x_sorted[:, i, :], rhs=stretch[:].rearrange("s c t -> s (c t)"), start=False, stop=True
+                    out=offset[:], lhsT=x_clamped[:, i, :], rhs=stretch[:].rearrange("s c t -> s (c t)"), start=False, stop=True
                 )
                 offset_of[i] = offset
 
@@ -275,7 +277,7 @@ def tile_conv2dkan_pa_kernel(tc, x, spline_kernel, scale_factor, base, kan_bias,
                 nc.scalar.activation(out=dist_of[i][:], in_=offset_of[i][:], func=ACT.Abs)
 
             def side(i):
-                side_of[i] = work.tile([P, TILE_VALUES], BF16, name="side")
+                side_of[i] = side_pool.tile([P, TILE_VALUES], BF16, name="side")
                 nc.scalar.activation(out=side_of[i][:], in_=offset_of[i][:], func=ACT.Sign)
 
             def distance(i):
@@ -333,33 +335,38 @@ def tile_conv2dkan_pa_kernel(tc, x, spline_kernel, scale_factor, base, kan_bias,
                 signed_of[i] = work.tile([P, TILE_VALUES], BF16, name="signed")
                 nc.vector.tensor_tensor(out=signed_of[i][:], in0=value_of[i][:], in1=side_of[i][:], op=ALU.mult)
 
-            def lower_half(i):
+            def spread_signed(i):
+                spread_of[i] = spread_psum.tile([P, HALVES, TILE_VALUES], BF16, name="spread_signed")
+                for half in range(HALVES):
+                    nc.tensor.matmul(
+                        out=spread_of[i][:, half, :],
+                        lhsT=spread[:, half, :, :].rearrange("c j h -> c (j h)"),
+                        rhs=signed_of[i][:],
+                        start=True,
+                        stop=True,
+                    )
+
+            def positive(i):
                 nc.vector.tensor_scalar(
-                    out=basis_bf[:, 0, i * TILE_VALUES : (i + 1) * TILE_VALUES],
-                    in0=signed_of[i][:],
+                    out=basis_bf[:, :, i * TILE_VALUES : (i + 1) * TILE_VALUES],
+                    in0=spread_of[i][:],
                     scalar1=0.0,
                     scalar2=None,
                     op0=ALU.max,
                 )
 
-            def upper_half(i):
-                nc.vector.tensor_scalar(
-                    out=basis_bf[:, 1, i * TILE_VALUES : (i + 1) * TILE_VALUES],
-                    in0=signed_of[i][:],
-                    scalar1=-1.0,
-                    scalar2=0.0,
-                    op0=ALU.mult,
-                    op1=ALU.max,
-                )
-
             offsets(0)
             offsets(1)
 
-            def add_biases(m):
-                total = rest_psum.tile([P, FEATURES], F32, name="total")
-                nc.tensor.matmul(out=total[:], lhsT=ident[:], rhs=base_sb[:, m, :], start=True, stop=False)
-                nc.tensor.matmul(out=total[:], lhsT=ones[:], rhs=bias_rows[:], start=False, stop=True)
-                nc.scalar.copy(out=rest[:, m, :], in_=total[:])
+            sum_of = {}
+
+            def sum_biases(m):
+                sum_of[m] = rest_psum.tile([P, FEATURES], F32, name="total")
+                nc.tensor.matmul(out=sum_of[m][:], lhsT=ident[:], rhs=base_sb[:, m, :], start=True, stop=False)
+                nc.tensor.matmul(out=sum_of[m][:], lhsT=ones[:], rhs=bias_rows[:], start=False, stop=True)
+
+            def keep_sum(m):
+                nc.scalar.copy(out=rest[:, m, :], in_=sum_of[m][:])
 
             for n in range(HEAD_SCALES):
                 scale_weights(n)
@@ -367,7 +374,7 @@ def tile_conv2dkan_pa_kernel(tc, x, spline_kernel, scale_factor, base, kan_bias,
                 return 0 <= i < X_TILES
 
             for step in range(X_TILES + STAGES - 1):
-                first, second, third, fourth = step, step - 1, step - 2, step - 3
+                first, second, third, fourth, fifth = step, step - 1, step - 2, step - 3, step - 4
                 if live(first + 2):
                     offsets(first + 2)
                 if live(first):
@@ -382,33 +389,37 @@ def tile_conv2dkan_pa_kernel(tc, x, spline_kernel, scale_factor, base, kan_bias,
                     distance(first)
                 if live(third):
                     outer(third)
+                if live(fourth):
+                    signed(fourth)
+                    spread_signed(fourth)
                 if live(third):
                     inner(third)
-                if live(fourth):
-                    lower_half(fourth)
+                if live(fifth):
+                    positive(fifth)
                 if live(third):
                     value(third)
-                if live(fourth):
-                    upper_half(fourth)
-                if live(third):
-                    signed(third)
-                if fourth == EARLY_TILES - 1:
-                    quantise_basis(0, (512, 256))
                 if step == X_TILES:
                     for n in range(HALVES):
                         regroup_weights(n)
+                if fifth == EARLY_TILES - 1:
+                    quantise_basis(0, (512, 256))
+                if fifth == EARLY_TILES:
                     for n in range(HALVES):
                         quantise_weights(n)
-                if fourth == MAIN_TILES - 1:
+                if fifth == MAIN_TILES - 1:
                     quantise_basis(EARLY_TILES * P, (256,))
                     for dj in range(1, TAPS_W):
                         shift_tap(dj)
-                if step == EDGE_SORT_STEP:
-                    sort_x(MAIN_TILES, X_TILES)
+                if step == X_TILES - 1:
+                    for m in range(EARLY_REST):
+                        sum_biases(m)
+                if step == X_TILES:
+                    for m in range(EARLY_REST):
+                        keep_sum(m)
+                if step == EDGE_CLAMP_STEP:
+                    clamp_x(MAIN_TILES, X_TILES)
                 if step in SCALE_STEPS:
                     scale_weights(HEAD_SCALES + SCALE_STEPS.index(step))
-            for m in range(EARLY_REST):
-                add_biases(m)
             for n in range(HALVES, LEAD):
                 regroup_weights(n)
             quantise_basis(MAIN, (128,))
@@ -440,7 +451,8 @@ def tile_conv2dkan_pa_kernel(tc, x, spline_kernel, scale_factor, base, kan_bias,
             if n + AHEAD < CHUNKS:
                 scale_weights(n + AHEAD)
             if 1 <= n <= OUT_TILES - EARLY_REST:
-                add_biases(EARLY_REST + n - 1)
+                sum_biases(EARLY_REST + n - 1)
+                keep_sum(EARLY_REST + n - 1)
             if n + LEAD < CHUNKS:
                 regroup_weights(n + LEAD)
             if n == HALVES - 1:

@@ -32,15 +32,14 @@ MAIN_TILES = MAIN // P
 TILE_VALUES = P * PACK
 OUT_TILES = ROWS_OUT // 2
 EARLY_TILES = 6
-EARLY_OUT = EARLY_TILES - 1
+REST_BANKS = 2
 CHUNKS = TAPS * HALVES
 GROUP = TAPS_H * HALVES
 RAW_BUFS = 8
-AHEAD = 4
-LEAD = 3
-VECTOR_EVERY = 9
+AHEAD = 3
+LEAD = 2
+VECTOR_EVERY = 5
 HEAD_SCALES = 2
-EARLY_REST = 1
 EDGE_CLAMP_STEP = 4
 SCALE_STEPS = (3, 4)
 STAGES = 5
@@ -55,8 +54,8 @@ def tile_conv2dkan_pa_kernel(tc, x, spline_kernel, scale_factor, base, kan_bias,
         work = ctx.enter_context(tc.tile_pool(name="work", bufs=3))
         side_pool = ctx.enter_context(tc.tile_pool(name="side", bufs=4))
         raw_pool = ctx.enter_context(tc.tile_pool(name="raw", bufs=RAW_BUFS))
-        scaled_pool = ctx.enter_context(tc.tile_pool(name="scaled", bufs=AHEAD + 1))
-        grouped_pool = ctx.enter_context(tc.tile_pool(name="grouped", bufs=LEAD + 1))
+        scaled_pool = ctx.enter_context(tc.tile_pool(name="scaled", bufs=AHEAD + 2))
+        grouped_pool = ctx.enter_context(tc.tile_pool(name="grouped", bufs=LEAD + 2))
         code_pool = ctx.enter_context(tc.tile_pool(name="code", bufs=4))
 
         ident = keep.tile([P, P], BF16)
@@ -170,7 +169,7 @@ def tile_conv2dkan_pa_kernel(tc, x, spline_kernel, scale_factor, base, kan_bias,
         codes_of = {}
 
         def by_vector(n):
-            return n % VECTOR_EVERY == VECTOR_EVERY - 1
+            return n > VECTOR_EVERY and n % VECTOR_EVERY == (CHUNKS - 1) % VECTOR_EVERY
 
         def scale_weights(n):
             if by_vector(n):
@@ -249,8 +248,10 @@ def tile_conv2dkan_pa_kernel(tc, x, spline_kernel, scale_factor, base, kan_bias,
                 in_=rows_of(basis_scales, MAIN, COLUMNS)[:, :, :, 0:dj],
             )
 
-        rest_psum = ctx.enter_context(tc.psum_pool(name="rest", bufs=1))
-        with tc.psum_pool(name="offsets", bufs=4) as offset_psum, tc.psum_pool(name="spread", bufs=2) as spread_psum:
+        with ExitStack() as phase:
+            offset_psum = phase.enter_context(tc.psum_pool(name="offsets", bufs=4))
+            spread_psum = phase.enter_context(tc.psum_pool(name="spread", bufs=2))
+            rest_psum = phase.enter_context(tc.psum_pool(name="rest", bufs=REST_BANKS))
             offset_of = {}
             dist_of = {}
             side_of = {}
@@ -399,28 +400,29 @@ def tile_conv2dkan_pa_kernel(tc, x, spline_kernel, scale_factor, base, kan_bias,
                 if live(third):
                     value(third)
                 if step == X_TILES:
+                    for m in range(OUT_TILES):
+                        keep_sum(m)
+                        if m + REST_BANKS < OUT_TILES:
+                            sum_biases(m + REST_BANKS)
                     for n in range(HALVES):
                         regroup_weights(n)
                 if fifth == EARLY_TILES - 1:
                     quantise_basis(0, (512, 256))
-                if fifth == EARLY_TILES:
-                    for n in range(HALVES):
-                        quantise_weights(n)
                 if fifth == MAIN_TILES - 1:
                     quantise_basis(EARLY_TILES * P, (256,))
+                    for n in range(HALVES):
+                        quantise_weights(n)
                     for dj in range(1, TAPS_W):
                         shift_tap(dj)
                 if step == X_TILES - 1:
-                    for m in range(EARLY_REST):
+                    for m in range(REST_BANKS):
                         sum_biases(m)
-                if step == X_TILES:
-                    for m in range(EARLY_REST):
-                        keep_sum(m)
                 if step == EDGE_CLAMP_STEP:
                     clamp_x(MAIN_TILES, X_TILES)
                 if step in SCALE_STEPS:
                     scale_weights(HEAD_SCALES + SCALE_STEPS.index(step))
-            for n in range(HALVES, LEAD):
+            scale_weights(HALVES + LEAD)
+            for n in range(HALVES, HALVES + LEAD):
                 regroup_weights(n)
             quantise_basis(MAIN, (128,))
 
@@ -443,26 +445,19 @@ def tile_conv2dkan_pa_kernel(tc, x, spline_kernel, scale_factor, base, kan_bias,
                 stop=(n == CHUNKS - 1),
             )
 
-        for n in range(CHUNKS):
-            if n >= HALVES:
-                quantise_weights(n)
+        for n in range(HALVES):
+            for m in range(OUT_TILES):
+                multiply(n, m)
+
+        for n in range(HALVES, CHUNKS):
+            quantise_weights(n)
             if n % GROUP == GROUP // 2 and n // GROUP + 1 < TAPS_W:
                 mend_tap(n // GROUP + 1)
             if n + AHEAD < CHUNKS:
                 scale_weights(n + AHEAD)
-            if 1 <= n <= OUT_TILES - EARLY_REST:
-                sum_biases(EARLY_REST + n - 1)
-                keep_sum(EARLY_REST + n - 1)
             if n + LEAD < CHUNKS:
                 regroup_weights(n + LEAD)
-            if n == HALVES - 1:
-                for early in range(HALVES):
-                    for m in range(EARLY_OUT):
-                        multiply(early, m)
-                for early in range(HALVES):
-                    for m in range(EARLY_OUT, OUT_TILES):
-                        multiply(early, m)
-            elif HALVES <= n < CHUNKS - HALVES:
+            if n < CHUNKS - HALVES:
                 for m in range(OUT_TILES):
                     multiply(n, m)
 
@@ -470,8 +465,12 @@ def tile_conv2dkan_pa_kernel(tc, x, spline_kernel, scale_factor, base, kan_bias,
             multiply(CHUNKS - 2, m)
             multiply(CHUNKS - 1, m)
             nc.vector.tensor_tensor(out=rest[:, m, :], in0=acc[m][:], in1=rest[:, m, :], op=ALU.add)
-            for b in range(IMAGES):
-                nc.sync.dma_start(
-                    out=out[b].rearrange("p q o -> (p q) o")[m * 32 : (m + 1) * 32, :],
-                    in_=rest[b:P:IMAGES, m, :],
-                )
+            if m % 2 == 1 or m == OUT_TILES - 1:
+                first = m - m % 2
+                for b in range(IMAGES):
+                    nc.sync.dma_start(
+                        out=out[b].rearrange("p q o -> (p q) o").rearrange("(m s) o -> s m o", s=P // IMAGES)[
+                            :, first : m + 1, :
+                        ],
+                        in_=rest[b:P:IMAGES, first : m + 1, :],
+                    )

import math
from contextlib import ExitStack

import concourse.mybir as mybir
from concourse.masks import make_identity

FP8X4 = mybir.dt.float8_e4m3fn_x4
BF16 = mybir.dt.bfloat16
F32 = mybir.dt.float32
I32 = mybir.dt.int32
U32 = mybir.dt.uint32
U8 = mybir.dt.uint8
ALU = mybir.AluOpType
ACT = mybir.ActivationFunctionType

P = 128
PACK = 4
IMAGES, ROWS_IN, COLS_IN, CHANNELS = 4, 16, 18, 128
ROWS_OUT, COLS_OUT, FEATURES = 14, 16, 512
TAPS_H, TAPS_W = 3, 3
TAPS = TAPS_H * TAPS_W
HALVES = 2
PASS_CHANNELS = CHANNELS // HALVES
WORDS = 2
COLUMNS = ROWS_IN * COLS_IN * IMAGES
ROW_WINDOW = COLS_OUT * IMAGES
MAIN = ROWS_IN * ROW_WINDOW
EDGE_PIXELS = COLS_IN - COLS_OUT
EDGE_WIDTH = EDGE_PIXELS * IMAGES
X_TILES = COLUMNS // P
MAIN_TILES = MAIN // P
TILE_VALUES = P * PACK
OUT_TILES = ROWS_OUT // 2
EARLY_TILES = 6
REST_BANKS = 2
CHUNKS = TAPS * HALVES
GROUP = TAPS_H * HALVES
RAW_BUFS = 8
AHEAD = 3
LEAD = 2
VECTOR_EVERY = 5
HEAD_SCALES = 2
EDGE_CLAMP_STEP = 4
SCALE_STEPS = (3, 4)
STAGES = 5
FLOPS = 2 * IMAGES * ROWS_OUT * COLS_OUT * TAPS * CHANNELS * 8 * FEATURES


def tile_conv2dkan_pa_kernel(tc, x, spline_kernel, scale_factor, base, kan_bias, conv_bias, out):
    nc = tc.nc
    with ExitStack() as ctx:
        ctx.enter_context(tc.manual_schedule())
        keep = ctx.enter_context(tc.tile_pool(name="keep", bufs=1))
        work = ctx.enter_context(tc.tile_pool(name="work", bufs=3))
        side_pool = ctx.enter_context(tc.tile_pool(name="side", bufs=4))
        raw_pool = ctx.enter_context(tc.tile_pool(name="raw", bufs=RAW_BUFS))
        scaled_pool = ctx.enter_context(tc.tile_pool(name="scaled", bufs=AHEAD + 2))
        grouped_pool = ctx.enter_context(tc.tile_pool(name="grouped", bufs=LEAD + 2))
        code_pool = ctx.enter_context(tc.tile_pool(name="code", bufs=4))

        ident = keep.tile([P, P], BF16)
        make_identity(nc, ident[:])

        x_sb = keep.tile([P, X_TILES, CHANNELS], BF16)
        for b in range(IMAGES):
            for r in range(2):
                (nc.sync if r == 0 else nc.scalar).dma_start(
                    out=x_sb[r * ROW_WINDOW + b : (r + 1) * ROW_WINDOW : IMAGES, 0:MAIN_TILES, :],
                    in_=x[b].rearrange("(i r) q c -> r q i c", r=2)[r, 0:COLS_OUT],
                )
        factors_first = keep.tile([P, HALVES, 1, FEATURES], BF16)
        factors_rest = keep.tile([P, HALVES, TAPS - 1, FEATURES], BF16)

        def load_factors(tile, first_tap, end_tap):
            rows = scale_factor.rearrange("(tap c) o -> c tap o", c=CHANNELS)
            for half in range(HALVES):
                for h in range(WORDS):
                    nc.sync.dma_start(
                        out=tile[h:P:WORDS, half, :, :],
                        in_=rows[half * PASS_CHANNELS : (half + 1) * PASS_CHANNELS, first_tap:end_tap, :],
                    )

        def factors_of(n):
            tap = tap_of(n)
            return factors_first[:, n % HALVES, 0, :] if tap == 0 else factors_rest[:, n % HALVES, tap - 1, :]

        raw_of = {}

        def tap_of(n):
            return ((n % GROUP) // HALVES) * TAPS_W + n // GROUP

        def load_weights(n):
            first = tap_of(n) * CHANNELS + n % HALVES * PASS_CHANNELS
            raw_of[n] = raw_pool.tile([P, PACK, FEATURES], BF16, name="raw")
            nc.sync.dma_start(
                out=raw_of[n][:], in_=spline_kernel[first : first + PASS_CHANNELS].rearrange("c (h t) o -> (c h) t o", h=WORDS)
            )

        load_factors(factors_first, 0, 1)
        for n in range(HALVES):
            load_weights(n)
        load_factors(factors_rest, 1, TAPS)
        for n in range(HALVES, 2 * HALVES):
            load_weights(n)
        for b in range(IMAGES):
            for e in range(EDGE_PIXELS):
                nc.sync.dma_start(out=x_sb[e * IMAGES + b : P : EDGE_WIDTH, MAIN_TILES, :], in_=x[b, :, COLS_OUT + e, :])
        bias_rows = keep.tile([P, FEATURES], BF16)
        nc.vector.memset(bias_rows[:], 0.0)
        nc.sync.dma_start(out=bias_rows[0:1, :], in_=kan_bias.rearrange("(a o) -> a o", a=1))
        nc.sync.dma_start(out=bias_rows[1:2, :], in_=conv_bias.rearrange("(a o) -> a o", a=1))
        base_sb = keep.tile([P, OUT_TILES, FEATURES], BF16)
        for b in range(IMAGES):
            nc.sync.dma_start(
                out=base_sb[b:P:IMAGES, :, :],
                in_=base[b].rearrange("p q o -> (p q) o").rearrange("(m s) o -> s m o", s=P // IMAGES),
            )

        for n in range(2 * HALVES, RAW_BUFS):
            load_weights(n)

        ones = keep.tile([P, P], BF16)
        nc.vector.memset(ones[:], 1.0)
        stretch = keep.tile([P, P, PACK], BF16)
        nc.vector.tensor_scalar(
            out=stretch[:], in0=ident[:].unsqueeze(2).to_broadcast([P, P, PACK]), scalar1=2.5, scalar2=None, op0=ALU.mult
        )
        shift = keep.tile([P, P, PACK], BF16)
        for t in range(PACK):
            nc.vector.memset(shift[:, :, t], (1.5 - t) / P)

        basis_bf = keep.tile([P, HALVES, COLUMNS * PACK], BF16, align_bytes=64)
        basis_codes = keep.tile([P, HALVES, COLUMNS], U32, align_bytes=64)
        basis_scales = keep.tile([P, HALVES, COLUMNS], U8, align_bytes=64)
        nc.vector.memset(basis_scales[:].bitcast(I32), 0)
        tap_codes = {
            dj: keep.tile([P, HALVES, MAIN], U32, name="tap_codes%d" % dj, align_bytes=64) for dj in range(1, TAPS_W)
        }
        tap_scales = {
            dj: keep.tile([P, HALVES, MAIN], U8, name="tap_scales%d" % dj, align_bytes=64) for dj in range(1, TAPS_W)
        }
        rest = keep.tile([P, OUT_TILES, FEATURES], F32)

        x_clamped = keep.tile([P, X_TILES, CHANNELS], BF16)

        def clamp_x(first_tile, end_tile):
            nc.vector.tensor_scalar(
                out=x_clamped[:, first_tile:end_tile, :],
                in0=x_sb[:, first_tile:end_tile, :],
                scalar1=-4.0,
                scalar2=4.0,
                op0=ALU.max,
                op1=ALU.min,
            )

        clamp_x(0, MAIN_TILES)
        spread = keep.tile([P, HALVES, PASS_CHANNELS, WORDS], BF16)
        for h in range(WORDS):
            nc.vector.tensor_scalar(
                out=spread[:, :, :, h],
                in0=ident[:].rearrange("c (half j) -> c half j", half=HALVES),
                scalar1=1.0 - 2.0 * h,
                scalar2=None,
                op0=ALU.mult,
            )

        scaled_of = {}
        grouped_of = {}
        codes_of = {}

        def by_vector(n):
            return n > VECTOR_EVERY and n % VECTOR_EVERY == (CHUNKS - 1) % VECTOR_EVERY

        def scale_weights(n):
            if by_vector(n):
                grouped = grouped_pool.tile([P, FEATURES, PACK], BF16, name="grouped", align_bytes=64)
                nc.vector.tensor_tensor(
                    out=grouped[:],
                    in0=raw_of[n][:].rearrange("p j o -> p o j"),
                    in1=factors_of(n).unsqueeze(2).to_broadcast([P, FEATURES, PACK]),
                    op=ALU.mult,
                )
                grouped_of[n] = grouped
            else:
                scaled = scaled_pool.tile([P, PACK, FEATURES], BF16, name="scaled")
                nc.vector.tensor_tensor(
                    out=scaled[:],
                    in0=raw_of[n][:],
                    in1=factors_of(n).unsqueeze(1).to_broadcast([P, PACK, FEATURES]),
                    op=ALU.mult,
                )
                scaled_of[n] = scaled
            if n + RAW_BUFS < CHUNKS:
                load_weights(n + RAW_BUFS)

        def regroup_weights(n):
            if not by_vector(n):
                grouped = grouped_pool.tile([P, FEATURES, PACK], BF16, name="grouped", align_bytes=64)
                nc.scalar.copy(
                    out=grouped[:].rearrange("p (c i) j -> p c j i", i=4),
                    in_=scaled_of[n][:].rearrange("p j (c i) -> p c j i", i=4),
                )
                grouped_of[n] = grouped

        def quantise_weights(n):
            w_codes = code_pool.tile([P, FEATURES], U32, name="w_codes", align_bytes=64)
            w_scales = code_pool.tile([P, FEATURES], U8, name="w_scales", align_bytes=64)
            nc.vector.quantize_mx(
                out=w_codes[:].bitcast(FP8X4),
                scales=w_scales[:],
                in_=grouped_of[n][:].rearrange("p o j -> p (o j)"),
            )
            codes_of[n] = (w_codes, w_scales)

        def quantise_basis(first_column, widths):
            for half in range(HALVES):
                first = first_column
                for width in widths:
                    nc.vector.quantize_mx(
                        out=basis_codes[:, half, first : first + width].bitcast(FP8X4),
                        scales=basis_scales[:, half, first : first + width],
                        in_=basis_bf[:, half, first * PACK : (first + width) * PACK],
                    )
                    first = first + width

        def rows_of(tile, first, end):
            return tile[:, :, first:end].bitcast(I32).rearrange("p h (r w) -> p h r w", r=ROWS_IN)

        def shift_tap(dj):
            shift_by = dj * IMAGES
            nc.sync.dma_start(
                out=tap_codes[dj][:, :, 0 : MAIN - shift_by].bitcast(I32),
                in_=basis_codes[:, :, shift_by:MAIN].bitcast(I32),
            )
            nc.sync.dma_start(
                out=tap_scales[dj][:, :, 0 : MAIN - shift_by].bitcast(I32),
                in_=basis_scales[:, :, shift_by:MAIN].bitcast(I32),
            )

        def mend_tap(dj):
            stay = COLS_OUT - dj
            nc.vector.tensor_copy(
                out=rows_of(tap_codes[dj], 0, MAIN)[:, :, :, stay * IMAGES : ROW_WINDOW],
                in_=rows_of(basis_codes, MAIN, COLUMNS)[:, :, :, 0 : dj * IMAGES],
            )
            nc.vector.tensor_copy(
                out=rows_of(tap_scales[dj], 0, MAIN)[:, :, :, stay:COLS_OUT],
                in_=rows_of(basis_scales, MAIN, COLUMNS)[:, :, :, 0:dj],
            )

        with ExitStack() as phase:
            offset_psum = phase.enter_context(tc.psum_pool(name="offsets", bufs=4))
            spread_psum = phase.enter_context(tc.psum_pool(name="spread", bufs=2))
            rest_psum = phase.enter_context(tc.psum_pool(name="rest", bufs=REST_BANKS))
            offset_of = {}
            dist_of = {}
            side_of = {}
            reach_of = {}
            square_of = {}
            outer_of = {}
            inner_of = {}
            value_of = {}
            signed_of = {}
            spread_of = {}

            def offsets(i):
                offset = offset_psum.tile([P, TILE_VALUES], F32, name="offset")
                nc.tensor.matmul(
                    out=offset[:], lhsT=ones[:], rhs=shift[:].rearrange("s c t -> s (c t)"), start=True, stop=False
                )
                nc.tensor.matmul(
                    out=offset[:], lhsT=x_clamped[:, i, :], rhs=stretch[:].rearrange("s c t -> s (c t)"), start=False, stop=True
                )
                offset_of[i] = offset

            def fold(i):
                dist_of[i] = work.tile([P, TILE_VALUES], F32, name="dist")
                nc.scalar.activation(out=dist_of[i][:], in_=offset_of[i][:], func=ACT.Abs)

            def side(i):
                side_of[i] = side_pool.tile([P, TILE_VALUES], BF16, name="side")
                nc.scalar.activation(out=side_of[i][:], in_=offset_of[i][:], func=ACT.Sign)

            def distance(i):
                nc.scalar.activation(out=dist_of[i][:], in_=dist_of[i][:], func=ACT.Abs, bias=-2.0, scale=1.0)

            def reach(i):
                reach_of[i] = work.tile([P, TILE_VALUES], F32, name="reach")
                nc.scalar.activation(out=reach_of[i][:], in_=dist_of[i][:], func=ACT.Relu, bias=2.0, scale=-1.0)

            def square(i):
                square_of[i] = work.tile([P, TILE_VALUES], F32, name="square")
                nc.scalar.activation(
                    out=square_of[i][:],
                    in_=dist_of[i][:],
                    func=ACT.Square,
                    bias=2.0 * math.sqrt(0.5),
                    scale=-math.sqrt(0.5),
                )

            def outer(i):
                outer_of[i] = work.tile([P, TILE_VALUES], F32, name="outer")
                nc.vector.scalar_tensor_tensor(
                    out=outer_of[i][:],
                    in0=reach_of[i][:],
                    scalar=-1.0 / 3.0,
                    in1=square_of[i][:],
                    op0=ALU.mult,
                    op1=ALU.mult,
                )

            def by_pairs(tile):
                return tile[:].rearrange("p (c h t) -> p c h t", h=2, t=2)

            def inner(i):
                inner_of[i] = work.tile([P, TILE_VALUES], F32, name="inner")
                nc.vector.tensor_tensor(
                    out=by_pairs(inner_of[i]),
                    in0=by_pairs(reach_of[i]),
                    in1=by_pairs(square_of[i])[:, :, ::-1, :],
                    op=ALU.mult,
                )

            def value(i):
                value_of[i] = work.tile([P, TILE_VALUES], BF16, name="value")
                nc.vector.scalar_tensor_tensor(
                    out=value_of[i][:],
                    in0=inner_of[i][:],
                    scalar=2.0 / 3.0,
                    in1=outer_of[i][:],
                    op0=ALU.subtract,
                    op1=ALU.max,
                )

            def signed(i):
                signed_of[i] = work.tile([P, TILE_VALUES], BF16, name="signed")
                nc.vector.tensor_tensor(out=signed_of[i][:], in0=value_of[i][:], in1=side_of[i][:], op=ALU.mult)

            def spread_signed(i):
                spread_of[i] = spread_psum.tile([P, HALVES, TILE_VALUES], BF16, name="spread_signed")
                for half in range(HALVES):
                    nc.tensor.matmul(
                        out=spread_of[i][:, half, :],
                        lhsT=spread[:, half, :, :].rearrange("c j h -> c (j h)"),
                        rhs=signed_of[i][:],
                        start=True,
                        stop=True,
                    )

            def positive(i):
                nc.vector.tensor_scalar(
                    out=basis_bf[:, :, i * TILE_VALUES : (i + 1) * TILE_VALUES],
                    in0=spread_of[i][:],
                    scalar1=0.0,
                    scalar2=None,
                    op0=ALU.max,
                )

            offsets(0)
            offsets(1)

            sum_of = {}

            def sum_biases(m):
                sum_of[m] = rest_psum.tile([P, FEATURES], F32, name="total")
                nc.tensor.matmul(out=sum_of[m][:], lhsT=ident[:], rhs=base_sb[:, m, :], start=True, stop=False)
                nc.tensor.matmul(out=sum_of[m][:], lhsT=ones[:], rhs=bias_rows[:], start=False, stop=True)

            def keep_sum(m):
                nc.scalar.copy(out=rest[:, m, :], in_=sum_of[m][:])

            for n in range(HEAD_SCALES):
                scale_weights(n)
            def live(i):
                return 0 <= i < X_TILES

            for step in range(X_TILES + STAGES - 1):
                first, second, third, fourth, fifth = step, step - 1, step - 2, step - 3, step - 4
                if live(first + 2):
                    offsets(first + 2)
                if live(first):
                    fold(first)
                if live(second):
                    reach(second)
                if live(first):
                    side(first)
                if live(second):
                    square(second)
                if live(first):
                    distance(first)
                if live(third):
                    outer(third)
                if live(fourth):
                    signed(fourth)
                    spread_signed(fourth)
                if live(third):
                    inner(third)
                if live(fifth):
                    positive(fifth)
                if live(third):
                    value(third)
                if step == X_TILES:
                    for m in range(OUT_TILES):
                        keep_sum(m)
                        if m + REST_BANKS < OUT_TILES:
                            sum_biases(m + REST_BANKS)
                    for n in range(HALVES):
                        regroup_weights(n)
                if fifth == EARLY_TILES - 1:
                    quantise_basis(0, (512, 256))
                if fifth == MAIN_TILES - 1:
                    quantise_basis(EARLY_TILES * P, (256,))
                    for n in range(HALVES):
                        quantise_weights(n)
                    for dj in range(1, TAPS_W):
                        shift_tap(dj)
                if step == X_TILES - 1:
                    for m in range(REST_BANKS):
                        sum_biases(m)
                if step == EDGE_CLAMP_STEP:
                    clamp_x(MAIN_TILES, X_TILES)
                if step in SCALE_STEPS:
                    scale_weights(HEAD_SCALES + SCALE_STEPS.index(step))
            scale_weights(HALVES + LEAD)
            for n in range(HALVES, HALVES + LEAD):
                regroup_weights(n)
            quantise_basis(MAIN, (128,))

        acc_pool = ctx.enter_context(tc.psum_pool(name="acc", bufs=1, reuse_waits="tile"))
        acc = [acc_pool.tile([P, FEATURES], F32, name="acc%d" % m) for m in range(OUT_TILES)]

        def multiply(n, m):
            half = n % HALVES
            di, dj = divmod(tap_of(n), TAPS_W)
            codes, scales = (tap_codes[dj], tap_scales[dj]) if dj > 0 else (basis_codes, basis_scales)
            window = slice((2 * m + di) * ROW_WINDOW, (2 * m + di) * ROW_WINDOW + P)
            w_codes, w_scales = codes_of[n]
            nc.tensor.matmul_mx(
                out=acc[m][:],
                lhsT=codes[:, half, window].bitcast(FP8X4),
                lhsT_scale=scales[:, half, window],
                rhs=w_codes[:].bitcast(FP8X4),
                rhs_scale=w_scales[:],
                start=(n == 0),
                stop=(n == CHUNKS - 1),
            )

        for n in range(HALVES):
            for m in range(OUT_TILES):
                multiply(n, m)

        for n in range(HALVES, CHUNKS):
            quantise_weights(n)
            if n % GROUP == GROUP // 2 and n // GROUP + 1 < TAPS_W:
                mend_tap(n // GROUP + 1)
            if n + AHEAD < CHUNKS:
                scale_weights(n + AHEAD)
            if n + LEAD < CHUNKS:
                regroup_weights(n + LEAD)
            if n < CHUNKS - HALVES:
                for m in range(OUT_TILES):
                    multiply(n, m)

        for m in range(OUT_TILES):
            multiply(CHUNKS - 2, m)
            multiply(CHUNKS - 1, m)
            nc.vector.tensor_tensor(out=rest[:, m, :], in0=acc[m][:], in1=rest[:, m, :], op=ALU.add)
            if m % 2 == 1 or m == OUT_TILES - 1:
                first = m - m % 2
                for b in range(IMAGES):
                    nc.sync.dma_start(
                        out=out[b].rearrange("p q o -> (p q) o").rearrange("(m s) o -> s m o", s=P // IMAGES)[
                            :, first : m + 1, :
                        ],
                        in_=rest[b:P:IMAGES, first : m + 1, :],
                    )
